import numpy as np
import ml_dtypes


def mxq(x, axis, fmt="e4m3"):
    dtype, down = {"e4m3": (ml_dtypes.float8_e4m3fn, 7), "e5m2": (ml_dtypes.float8_e5m2, 14)}[fmt]
    v = np.moveaxis(np.asarray(x, np.float32).astype(ml_dtypes.bfloat16).astype(np.float64), axis, -1)
    blocks = v.reshape(v.shape[:-1] + (-1, 32))
    amax = np.abs(blocks).max(-1, keepdims=True)
    byte = np.maximum(np.where(amax > 0, np.frexp(amax)[1] - 1 + 127, 0) - down, 1)
    scale = np.exp2(byte - 127.0)
    codes = (blocks / scale).astype(np.float32).astype(dtype).astype(np.float64)
    return np.moveaxis((codes * scale).reshape(v.shape), -1, axis)


WIDE = False


def mx_kscale(k):
    if not WIDE:
        return np.ones(k)
    levels = np.array([18, -18])
    if k % 512:
        return np.exp2(np.random.permutation(np.resize(levels, k // 32))).repeat(32)
    a = np.empty((k // 512, 16))
    for p in range(k // 512):
        a[p, :8] = np.random.permutation(np.resize(levels, 8))
        for g in range(8):
            far = levels[np.abs(levels - a[p, g]) >= 10]
            a[p, g + 8] = far[np.random.randint(len(far))]
    return np.exp2(a.ravel()).repeat(32)


BF16 = ml_dtypes.bfloat16


def bf(x):
    return np.asarray(x, np.float32).astype(BF16)


def f64(x):
    return np.asarray(x).astype(np.float64)


B, T, C, D = 2, 512, 1024, 512
ROPE_BASE = 10000.0


def rotate_half(u):
    u1, u2 = np.split(u, 2, axis=-1)
    return np.concatenate([-u2, u1], axis=-1)


def rope_tables():
    inv_freq = 1.0 / (ROPE_BASE ** (f64(np.arange(0, D, 2)) / D))
    freqs = f64(np.arange(T))[:, None] * inv_freq[None, :]
    emb = np.concatenate([freqs, freqs], -1)
    return np.cos(emb), np.sin(emb)


def norm_rope_backward(g, u, gain, cos, sin):
    r = 1.0 / np.sqrt((u * u).sum(-1, keepdims=True))
    n = u * r
    dn = g * gain
    du = r * (dn - n * (dn * n).sum(-1, keepdims=True))
    return du * cos - rotate_half(du * sin)


def setup_inputs():
    s = mx_kscale(B * T).reshape(B, T, 1)
    u = mx_kscale(3 * D)
    uq = np.full(D, u[0])
    uk = np.full(D, 1.0 / u[0])
    uv = u[2 * D:]
    uj = np.concatenate([uq, uk, uv])
    x0 = bf(np.random.standard_normal((B, T, C)))
    w0 = bf(np.random.standard_normal((3 * D, C)) / np.sqrt(C))
    sqk = bf(0.75 * (1.0 + 0.25 * np.random.standard_normal(D)))
    g0 = bf(30.0 * np.random.standard_normal((B, T, D)) * np.exp2(np.random.randint(-6, 1, (B, T, 1))) / s * uq)
    g1 = bf(30.0 * np.random.standard_normal((B, T, D)) * np.exp2(np.random.randint(-6, 1, (B, T, 1))) / s * uk)
    g2 = bf(np.random.standard_normal((B, T, D)) * np.exp2(np.random.randint(-6, 1, (B, T, 1))) / s * uv)
    qkv = f64(x0) @ f64(w0).T
    q0, k0, v0 = np.split(qkv, 3, axis=-1)
    cos, sin = rope_tables()
    q1 = q0 * cos + rotate_half(q0) * sin
    k1 = k0 * cos + rotate_half(k0) * sin
    return {"x": bf(f64(x0) * s), "W_qkv": bf(f64(w0) / uj[:, None]), "sqk": sqk,
            "q1": np.asarray(q1, np.float32), "k1": np.asarray(k1, np.float32),
            "grad_0": g0, "grad_1": g1, "grad_2": g2}


def reference(x, W_qkv, sqk, q1, k1, grad_0, grad_1, grad_2):
    cos, sin = rope_tables()
    gain = f64(sqk)
    dq = norm_rope_backward(f64(grad_0), f64(q1), gain, cos, sin)
    dk = norm_rope_backward(f64(grad_1), f64(k1), gain, cos, sin)
    dz = np.concatenate([dq, dk, f64(grad_2)], axis=-1).reshape(B * T, 3 * D)
    xf = f64(x).reshape(B * T, C)
    dx = mxq(dz, 1, "e5m2") @ mxq(f64(W_qkv), 0, "e4m3")
    dw = mxq(dz, 0, "e5m2").T @ mxq(xf, 0, "e4m3")
    return dx.reshape(B, T, C), dw

@@ -1,0 +1,432 @@
+import math
+from contextlib import ExitStack
+
+import concourse.mybir as mybir
+from concourse.masks import make_identity
+
+F32 = mybir.dt.float32
+BF16 = mybir.dt.bfloat16
+I32 = mybir.dt.int32
+U32 = mybir.dt.uint32
+U8 = mybir.dt.uint8
+E4M3 = mybir.dt.float8_e4m3fn_x4
+E5M2 = mybir.dt.float8_e5m2_x4
+ALU = mybir.AluOpType
+ACT = mybir.ActivationFunctionType
+
+P = 128
+J = 4
+B, T, C, D = 2, 512, 1024, 512
+H = D // 2
+ROPE_BASE = 10000.0
+FLOPS = 2 * 2 * (B * T) * (3 * D) * C
+
+UNITS = [(0, 0), (0, 1), (1, 0), (1, 1)]
+STEPS = 2 * len(UNITS)
+
+
+def tile_attentionhead_pa_v_kernel(tc, x, W_qkv, sqk, q1, k1, grad_0, grad_1, grad_2, out_0, out_1):
+    nc = tc.nc
+    saved = [q1, k1]
+    grads = [grad_0, grad_1, grad_2]
+
+    with ExitStack() as ctx:
+        keep = ctx.enter_context(tc.tile_pool(name="keep", bufs=1))
+        work = ctx.enter_context(tc.tile_pool(name="work", bufs=2))
+        ps_h = ctx.enter_context(tc.psum_pool(name="ps_h", bufs=2))
+        ps_t = ctx.enter_context(tc.psum_pool(name="ps_t", bufs=2))
+        ps_mx = ctx.enter_context(tc.psum_pool(name="ps_mx", bufs=4))
+        ctx.enter_context(tc.manual_schedule())
+
+        zrow = keep.tile([P, D], BF16, name="zrow")
+        nc.vector.memset(zrow[:], 0.0)
+        ones = keep.tile([P, P], BF16, name="ones")
+        nc.vector.memset(ones[:], 1.0)
+        pos = keep.tile([P, J], F32, name="pos")
+        nc.gpsimd.iota(pos[:], [[1, J]], base=0, channel_multiplier=J, allow_small_or_imprecise_dtypes=True)
+        ident_b = keep.tile([P, P], BF16, name="ident_b")
+        make_identity(nc, ident_b[:])
+        ident_f = keep.tile([P, P], F32, name="ident_f")
+        make_identity(nc, ident_f[:])
+        power = keep.tile([P, 2], F32, name="power")
+        nc.gpsimd.memset(power[:], -0.5)
+
+        g_t, u_t, g2_t, x_t, w_t = {}, {}, {}, {}, {}
+
+        def load_g(n):
+            s, b = UNITS[n]
+            g_t[n] = work.tile([P, J, D], BF16, tag="g", name="g", bufs=2)
+            nc.sync.dma_start(out=g_t[n][:], in_=grads[s][b].rearrange("(p j) w -> p j w", j=J))
+
+        def load_u(n, parts):
+            s, b = UNITS[n]
+            u_t[n] = work.tile([P, J, D], F32, tag="u", name="u", bufs=3)
+            view = saved[s][b].rearrange("(p j) w -> p j w", j=J)
+            w = J // parts
+            for h in range(parts):
+                nc.sync.dma_start(out=u_t[n][:, h * w : (h + 1) * w, :], in_=view[:, h * w : (h + 1) * w, :])
+
+        def load_g2(b):
+            g2_t[b] = work.tile([P, J, D], BF16, tag="g2", name="g2", bufs=2)
+            nc.sync.dma_start(out=g2_t[b][:], in_=grad_2[b].rearrange("(p j) w -> p j w", j=J))
+
+        def load_x(b):
+            x_t[b] = work.tile([P, J, C], BF16, tag="x", name="x_in", bufs=2)
+            nc.sync.dma_start(out=x_t[b][:], in_=x[b].rearrange("(p j) c -> p j c", j=J))
+
+        def load_w(s):
+            w_t[s] = work.tile([P, J, C], BF16, tag="w", name="w_in", bufs=2)
+            nc.sync.dma_start(out=w_t[s][:], in_=W_qkv[s * D : (s + 1) * D, :].rearrange("(p j) c -> p j c", j=J))
+
+        load_g(0)
+        nc.sync.dma_start(out=zrow[0:1, :], in_=sqk.rearrange("(o n) -> o n", o=1))
+        load_u(0, 2)
+        load_x(0)
+        load_g(1)
+        load_u(1, 1)
+        load_g2(0)
+        load_x(1)
+        load_g2(1)
+        load_w(2)
+        load_g(2)
+        load_u(2, 1)
+        load_w(0)
+        load_g(3)
+        load_u(3, 1)
+        load_w(1)
+
+        freq = keep.tile([P, H], F32, name="freq")
+        nc.vector.tensor_scalar(out=freq[:, 0:1], in0=pos[:, 0:1], scalar1=0.0, scalar2=1.0 / (2.0 * math.pi), op0=ALU.mult, op1=ALU.add)
+        for k in range(8):
+            n = 1 << k
+            nc.vector.tensor_scalar_mul(freq[:, n : 2 * n], freq[:, 0:n], ROPE_BASE ** (-float(n) / H))
+        tau = work.tile([P, J, H], F32, tag="A", name="tau")
+        for j in range(J):
+            nc.vector.tensor_scalar_mul(tau[:, j, :], freq[:], pos[:, j : j + 1])
+        whole = work.tile([P, J, H], I32, tag="B", name="whole")
+        nc.vector.tensor_copy(out=whole[:], in_=tau[:])
+        frac = work.tile([P, J, H], F32, tag="A", name="frac")
+        nc.vector.tensor_tensor(out=frac[:], in0=tau[:], in1=whole[:], op=ALU.subtract)
+        sin_t = keep.tile([P, J, H], F32, name="sin_t")
+        cos_t = keep.tile([P, J, H], F32, name="cos_t")
+        mag = work.tile([P, J, H], F32, tag="B", name="mag")
+        warm = keep.tile([P, 1], F32, name="warm")
+        nc.scalar.activation(out=warm[:], in_=pos[:, 0:1], func=ACT.Sin, scale=0.0)
+
+        def tables():
+            nc.scalar.activation(out=mag[:], in_=frac[:], func=ACT.Abs)
+            nc.scalar.activation(out=cos_t[:], in_=mag[:], func=ACT.Sin, scale=-2.0 * math.pi, bias=math.pi / 2.0)
+            nc.scalar.activation(out=sin_t[:], in_=frac[:], func=ACT.Sin, scale=2.0 * math.pi)
+
+        gain_ps = ps_h.tile([P, D], F32, tag="h", name="gain_ps")
+        nc.tensor.matmul(gain_ps[:], lhsT=ones[:], rhs=zrow[:], start=True, stop=True)
+        diag = keep.tile([P, 4, P], BF16, name="diag")
+        nc.vector.tensor_tensor(
+            out=diag[:],
+            in0=ident_b[:].unsqueeze(1).to_broadcast([P, 4, P]),
+            in1=gain_ps[:].rearrange("p (f n) -> p f n", f=4),
+            op=ALU.mult,
+        )
+
+        def codes(tag, width):
+            c = keep.tile([P, width], U32, name=tag + "_c", align_bytes=64)
+            s = keep.tile([P, width], U8, name=tag + "_s", align_bytes=64)
+            return c, s
+
+        x_q = [codes("x%d" % b, C) for b in range(B)]
+        w_q = [codes("w%d" % s, C) for s in range(3)]
+        tok_q = [[codes("t%d%d" % (s, b), D) for b in range(B)] for s in range(3)]
+        fea_q = [[codes("f%d%d" % (s, b), D) for b in range(B)] for s in range(3)]
+
+        def quantize(dst, lo, width, stage, fmt):
+            nc.vector.quantize_mx(
+                out=dst[0][:, lo : lo + width].bitcast(fmt),
+                scales=dst[1][:, lo : lo + width],
+                in_=stage,
+            )
+
+        def interleave(copy, dst, src):
+            copy(out=dst.rearrange("p (c i t) -> p c t i", i=4, t=J), in_=src.rearrange("p t (c i) -> p c t i", i=4))
+
+        staged = {}
+
+        def stage_piece(copy, key):
+            kind, a, n = key
+            st = work.tile([P, J * D], BF16, tag="stage", name="stage", bufs=5, align_bytes=64)
+            if kind == "x":
+                src = x_t[a][:, :, n * D : (n + 1) * D]
+            elif kind == "w":
+                src = w_t[a][:, :, n * D : (n + 1) * D]
+            elif kind == "v":
+                src = g2_t[n][:]
+            else:
+                src = z_t[a][:]
+            interleave(copy, st[:], src)
+            staged[key] = st
+
+        def quant_piece(key):
+            kind, a, n = key
+            st = staged[key]
+            if kind == "x":
+                quantize(x_q[a], n * D, D, st[:], E4M3)
+            elif kind == "w":
+                quantize(w_q[a], n * D, D, st[:], E4M3)
+            elif kind == "v":
+                quantize(tok_q[2][n], 0, D, st[:], E5M2)
+            else:
+                s, b = UNITS[a]
+                quantize(tok_q[s][b], 0, D, st[:], E5M2)
+
+        z_t, gT, h_t, ss, rr, rt, dots, nal, d_t, a_t, b_t = {}, {}, {}, {}, {}, {}, {}, {}, {}, {}, {}
+
+        def grad_transpose(i, copy=nc.scalar.copy):
+            tr = ps_t.tile([P, 2, 4, P], BF16, tag="tr", name="gtr")
+            for jj in range(2):
+                for f in range(4):
+                    nc.tensor.transpose(tr[:, jj, f, :], g_t[i // 2][:, 2 * (i % 2) + jj, f * P : (f + 1) * P], ident_b[:])
+            gT[i] = work.tile([P, 2, 4, P], BF16, tag="gT", name="gT", bufs=2)
+            copy(out=gT[i][:], in_=tr[:])
+
+        def gain(i):
+            for jj in range(2):
+                h = ps_h.tile([P, D], F32, tag="h", name="h")
+                for f in range(4):
+                    nc.tensor.matmul(h[:, f * P : (f + 1) * P], lhsT=gT[i][:, jj, f, :], rhs=diag[:, f, :], start=True, stop=True)
+                h_t[i, jj] = h
+
+        def squares(i):
+            ss[i] = work.tile([P, 2], F32, tag="ss", name="ss", bufs=3)
+            for jj in range(2):
+                sq = work.tile([P, D], BF16, tag="sq", name="sq")
+                nc.scalar.activation(out=sq[:], in_=u_t[i // 2][:, 2 * (i % 2) + jj, :], func=ACT.Square, accum_out=ss[i][:, jj : jj + 1])
+
+        def recip(i):
+            rr[i] = work.tile([P, 2], F32, tag="rr", name="rr", bufs=3)
+            nc.vector.reciprocal(rr[i][:], ss[i][:])
+
+        def root(i):
+            rt[i] = work.tile([P, 2], F32, tag="rt", name="rt", bufs=3)
+            nc.gpsimd.tensor_tensor(out=rt[i][:], in0=ss[i][:], in1=power[:], op=ALU.pow)
+
+        def dot(i, jj):
+            if jj == 0:
+                dots[i] = work.tile([P, 2], F32, tag="dots", name="dots", bufs=3)
+            prod = work.tile([P, D], F32, tag="prod", name="prod")
+            nc.vector.scalar_tensor_tensor(
+                out=prod[:], in0=h_t[i, jj][:], scalar=1.0, in1=u_t[i // 2][:, 2 * (i % 2) + jj, :],
+                op0=ALU.mult, op1=ALU.mult, accum_out=dots[i][:, jj : jj + 1],
+            )
+
+        def alpha(i):
+            nal[i] = work.tile([P, 2], F32, tag="nal", name="nal", bufs=3)
+            nc.vector.scalar_tensor_tensor(out=nal[i][:], in0=dots[i][:], scalar=-1.0, in1=rr[i][:], op0=ALU.mult, op1=ALU.mult)
+
+        def project(i, jj):
+            if jj == 0:
+                d_t[i] = work.tile([P, 2, D], F32, tag="d", name="d")
+            nc.vector.scalar_tensor_tensor(
+                out=d_t[i][:, jj, :], in0=u_t[i // 2][:, 2 * (i % 2) + jj, :], scalar=nal[i][:, jj : jj + 1], in1=h_t[i, jj][:],
+                op0=ALU.mult, op1=ALU.add,
+            )
+
+        def times(i, jj, table, store, tag):
+            if jj == 0:
+                store[i] = work.tile([P, 2, D], F32, tag=tag, name=tag)
+            nc.vector.scalar_tensor_tensor(
+                out=store[i][:, jj, :].rearrange("p (h w) -> p h w", h=2),
+                in0=d_t[i][:, jj, :].rearrange("p (h w) -> p h w", h=2),
+                scalar=rt[i][:, jj : jj + 1],
+                in1=table[:, 2 * (i % 2) + jj, :].unsqueeze(1).to_broadcast([P, 2, H]),
+                op0=ALU.mult, op1=ALU.mult,
+            )
+
+        def rotate(i):
+            if i % 2 == 0:
+                z_t[i // 2] = work.tile([P, J, D], BF16, tag="z", name="z", align_bytes=64)
+            js = slice(2 * (i % 2), 2 * (i % 2) + 2)
+            z, a, b = z_t[i // 2], a_t[i], b_t[i]
+            nc.vector.tensor_tensor(out=z[:, js, 0:H], in0=a[:, :, 0:H], in1=b[:, :, H:D], op=ALU.add)
+            nc.vector.tensor_tensor(out=z[:, js, H:D], in0=a[:, :, H:D], in1=b[:, :, 0:H], op=ALU.subtract)
+
+        fst = {}
+
+        def fea_transpose(key, copy=nc.scalar.copy):
+            if isinstance(key, int):
+                src, half = z_t[key // 2], key % 2
+            else:
+                src, half = g2_t[key[1]], key[2]
+            words = src[:].rearrange("p j w -> p (j w)").bitcast(F32)
+            tr = ps_t.tile([P, 2, 2, P], F32, tag="tr", name="ztr")
+            for jj in range(2):
+                lo = (2 * half + jj) * H
+                for e in range(2):
+                    nc.tensor.transpose(tr[:, jj, e, :], words[:, lo + e : lo + H : 2], ident_f[:])
+            fst[key] = work.tile([P, J * H], BF16, tag="fst", name="fst", bufs=3, align_bytes=64)
+            copy(
+                out=fst[key][:].bitcast(F32).rearrange("p (j t e) -> p j t e", j=2, e=2),
+                in_=tr[:].rearrange("p j e t -> p j t e"),
+            )
+
+        def fea_quant(key):
+            if isinstance(key, int):
+                s, b = UNITS[key // 2]
+                half = key % 2
+            else:
+                s, b, half = 2, key[1], key[2]
+            quantize(fea_q[s][b], half * H, H, fst[key][:], E5M2)
+
+        def passes(accs, lhs, rhs, lo, which, count):
+            for n in range(2):
+                for k in which:
+                    nc.tensor.matmul_mx(
+                        out=accs[n][:],
+                        lhsT=lhs[k][0][:, lo : lo + P].bitcast(E5M2),
+                        lhsT_scale=lhs[k][1][:, lo : lo + P],
+                        rhs=rhs[k][0][:, n * D : (n + 1) * D].bitcast(E4M3),
+                        rhs_scale=rhs[k][1][:, n * D : (n + 1) * D],
+                        start=(k == 0),
+                        stop=(k == count - 1),
+                    )
+
+        def accs_of(pool, tag):
+            a0 = pool.tile([P, D], F32, tag=tag, name="acc0")
+            a1 = pool.tile([P, D], F32, tag=tag, name="acc1")
+            return a0, a1
+
+        def empty(accs, dest, engines):
+            o = work.tile([P, C], F32, tag="o", name="o", bufs=5)
+            for n in range(2):
+                engines[n](out=o[:, n * D : (n + 1) * D], in_=accs[n][:])
+            nc.sync.dma_start(out=dest, in_=o[:])
+
+        def operands(item):
+            kind, a, n = item
+            if kind == "w":
+                r = a * D + n * P
+                return tok_q[a], x_q, n * P, out_1[r : r + P, :]
+            view = out_0[a].rearrange("(p j) c -> p j c", j=J)
+            return [fea_q[s][a] for s in (2, 0, 1)], [w_q[s] for s in (2, 0, 1)], n * P, view[:, n, :]
+
+        def mx_begin(item, pool, tag):
+            lhs, rhs, lo, dest = operands(item)
+            accs = accs_of(pool, tag)
+            passes(accs, lhs, rhs, lo, range(len(lhs) - 1), len(lhs))
+            return accs
+
+        def mx_finish(item, accs, engines):
+            lhs, rhs, lo, dest = operands(item)
+            passes(accs, lhs, rhs, lo, [len(lhs) - 1], len(lhs))
+            empty(accs, dest, engines)
+
+        def do_mx(item, engines):
+            lhs, rhs, lo, dest = operands(item)
+            accs = accs_of(ps_mx, "mx")
+            passes(accs, lhs, rhs, lo, range(len(lhs)), len(lhs))
+            empty(accs, dest, engines)
+
+        sc, ve = nc.scalar.copy, nc.vector.tensor_copy
+
+        s_fill = {
+            0: [("x", 0, 0), ("x", 0, 1), ("v", 0, 0)],
+            1: [("x", 1, 0), ("x", 1, 1), ("v", 0, 1)],
+            2: [("w", 2, 0)],
+            3: [("w", 2, 1), ("w", 0, 0)],
+            4: [("w", 0, 1), ("w", 1, 0)],
+        }
+        v_fill = {
+            2: [("z", 0, 0)],
+            4: [("z", 1, 0)],
+            5: [("w", 1, 1)],
+            6: [("z", 2, 0)],
+        }
+        mx_plan = {
+            3: [("w", 2, 0), ("w", 2, 1)],
+            4: [("w", 2, 2), ("w", 2, 3)],
+            5: [("w", 0, 0), ("w", 0, 1)],
+            6: [("w", 0, 2), ("w", 0, 3), ("x", 0, 0), ("x", 0, 1)],
+            7: [("x", 0, 2), ("x", 0, 3), ("x", 1, 0)],
+            8: [("x", 1, 1)],
+        }
+        v_feats = {1: [("v", 0, 0), ("v", 0, 1)], 3: [("v", 1, 0), ("v", 1, 1)]}
+
+        grad_transpose(0)
+        grad_transpose(1, nc.vector.tensor_copy)
+        squares(0)
+        gain(0)
+        dot(0, 0)
+        dot(0, 1)
+        recip(0)
+        tables()
+        squares(1)
+        alpha(0)
+        project(0, 0)
+        project(0, 1)
+        root(0)
+        gain(1)
+
+        pending = []
+        for i in range(STEPS):
+            nxt, pre = i + 1, i + 2
+            if i > 0:
+                fea_transpose(i - 1)
+            if pre < STEPS:
+                grad_transpose(pre)
+            for key in v_feats.get(i, []):
+                fea_transpose(key)
+            if nxt < STEPS:
+                dot(nxt, 0)
+                recip(nxt)
+                root(nxt)
+                dot(nxt, 1)
+            if pre < STEPS:
+                squares(pre)
+            times(i, 0, cos_t, a_t, "A")
+            if nxt < STEPS:
+                alpha(nxt)
+            times(i, 1, cos_t, a_t, "A")
+            times(i, 0, sin_t, b_t, "B")
+            if nxt < STEPS:
+                project(nxt, 0)
+            times(i, 1, sin_t, b_t, "B")
+            if nxt < STEPS:
+                project(nxt, 1)
+            if i < 7:
+                for item in mx_plan.get(i, []):
+                    do_mx(item, (sc, sc))
+            if pre < STEPS:
+                gain(pre)
+            for key in v_fill.get(i, []):
+                stage_piece(ve, key)
+            if i > 0:
+                fea_quant(i - 1)
+            for key in v_feats.get(i, []):
+                fea_quant(key)
+            if i == 7:
+                for item in mx_plan.get(i, []):
+                    do_mx(item, (sc, sc))
+            rotate(i)
+            for key in pending + v_fill.get(i, []):
+                quant_piece(key)
+            pending = s_fill.get(i, [])
+            for key in pending:
+                stage_piece(sc, key)
+
+        fea_transpose(STEPS - 1, ve)
+        for item in mx_plan[STEPS]:
+            do_mx(item, (sc, sc))
+        open_groups = [
+            (("x", 1, 2), mx_begin(("x", 1, 2), ps_mx, "mx")),
+            (("x", 1, 3), mx_begin(("x", 1, 3), ps_mx, "mx")),
+            (("w", 1, 0), mx_begin(("w", 1, 0), ps_h, "h")),
+        ]
+        st = work.tile([P, J * D], BF16, tag="stage", name="stage", bufs=5, align_bytes=64)
+        for m in range(4):
+            cols = slice(m * P, (m + 1) * P)
+            interleave(ve if m < 3 else sc, st[:, m * D : (m + 1) * D], z_t[3][:, :, cols])
+        fea_quant(STEPS - 1)
+        for m in range(4):
+            quantize(tok_q[1][1], m * P, P, st[:, m * D : (m + 1) * D], E5M2)
+        for item, accs in open_groups:
+            mx_finish(item, accs, (sc, ve))
+        for m in range(1, 4):
+            do_mx(("w", 1, m), (sc, ve))

@@ -24,6 +24,23 @@ FLOPS = 2 * 2 * (B * T) * (3 * D) * C
 UNITS = [(0, 0), (0, 1), (1, 0), (1, 1)]
 STEPS = 2 * len(UNITS)
 
+PLAN = {'e': {0: [('s', ('v', 0, 0))], 1: [('s', ('v', 0, 1))], 3: [('s', ('x', 1, 1))], 4: [('p', ('z', 0, 0))]},
+ 'finish': [('w', 1, 0), ('w', 1, 2), ('w', 1, 1), ('x', 1, 3), ('x', 1, 2), ('w', 1, 3)],
+ 'g': [('x', 0, 0), ('w', 0, 0), ('w', 1, 0)],
+ 'mx': {3.5: [('w', 2, 0, 0)],
+        4.5: [('w', 2, 3, 0)],
+        5: [('w', 2, 2, 0), ('w', 2, 1, 0), ('w', 0, 3, 0)],
+        6.5: [('w', 0, 0, 0), ('w', 0, 1, 0), ('w', 0, 2, 0), ('x', 0, 1, 0), ('x', 0, 0, 0)],
+        7: [('x', 0, 3, 0)],
+        7.5: [('x', 1, 0, 1), ('x', 1, 1, 0), ('x', 0, 2, 0)]},
+ 'open': [(('x', 1, 2), 'h'), (('w', 1, 0), 'mx'), (('w', 1, 2), 'mx')],
+ 's': {0: [('p', ('x', 0, 1))],
+       1: [('p', ('x', 1, 0))],
+       2: [('s', ('w', 2, 1)), ('s', ('w', 2, 0))],
+       3: [('p', ('z', 1, 0))],
+       4: [('s', ('w', 1, 1)), ('p', ('w', 0, 1))]},
+ 'v': {7: [('z', 2, 0)]}}
+
 
 def tile_attentionhead_pa_v_kernel(tc, x, W_qkv, sqk, q1, k1, grad_0, grad_1, grad_2, out_0, out_1):
     nc = tc.nc
@@ -48,23 +65,18 @@ def tile_attentionhead_pa_v_kernel(tc, x, W_qkv, sqk, q1, k1, grad_0, grad_1, gr
         make_identity(nc, ident_b[:])
         ident_f = keep.tile([P, P], F32, name="ident_f")
         make_identity(nc, ident_f[:])
-        power = keep.tile([P, 2], F32, name="power")
-        nc.gpsimd.memset(power[:], -0.5)
 
         g_t, u_t, g2_t, x_t, w_t = {}, {}, {}, {}, {}
 
-        def load_g(n):
+        def load_unit(n, parts):
             s, b = UNITS[n]
             g_t[n] = work.tile([P, J, D], BF16, tag="g", name="g", bufs=2)
-            nc.sync.dma_start(out=g_t[n][:], in_=grads[s][b].rearrange("(p j) w -> p j w", j=J))
-
-        def load_u(n, parts):
-            s, b = UNITS[n]
             u_t[n] = work.tile([P, J, D], F32, tag="u", name="u", bufs=3)
-            view = saved[s][b].rearrange("(p j) w -> p j w", j=J)
             w = J // parts
             for h in range(parts):
-                nc.sync.dma_start(out=u_t[n][:, h * w : (h + 1) * w, :], in_=view[:, h * w : (h + 1) * w, :])
+                for t, src in ((g_t[n], grads[s]), (u_t[n], saved[s])):
+                    view = src[b].rearrange("(p j) w -> p j w", j=J)
+                    nc.sync.dma_start(out=t[:, h * w : (h + 1) * w, :], in_=view[:, h * w : (h + 1) * w, :])
 
         def load_g2(b):
             g2_t[b] = work.tile([P, J, D], BF16, tag="g2", name="g2", bufs=2)
@@ -78,21 +90,17 @@ def tile_attentionhead_pa_v_kernel(tc, x, W_qkv, sqk, q1, k1, grad_0, grad_1, gr
             w_t[s] = work.tile([P, J, C], BF16, tag="w", name="w_in", bufs=2)
             nc.sync.dma_start(out=w_t[s][:], in_=W_qkv[s * D : (s + 1) * D, :].rearrange("(p j) c -> p j c", j=J))
 
-        load_g(0)
         nc.sync.dma_start(out=zrow[0:1, :], in_=sqk.rearrange("(o n) -> o n", o=1))
-        load_u(0, 2)
+        load_unit(0, 2)
         load_x(0)
-        load_g(1)
-        load_u(1, 1)
+        load_unit(1, 1)
         load_g2(0)
         load_x(1)
         load_g2(1)
         load_w(2)
-        load_g(2)
-        load_u(2, 1)
+        load_unit(2, 1)
         load_w(0)
-        load_g(3)
-        load_u(3, 1)
+        load_unit(3, 1)
         load_w(1)
 
         freq = keep.tile([P, H], F32, name="freq")
@@ -110,11 +118,11 @@ def tile_attentionhead_pa_v_kernel(tc, x, W_qkv, sqk, q1, k1, grad_0, grad_1, gr
         sin_t = keep.tile([P, J, H], F32, name="sin_t")
         cos_t = keep.tile([P, J, H], F32, name="cos_t")
         mag = work.tile([P, J, H], F32, tag="B", name="mag")
+        nc.vector.scalar_tensor_tensor(out=mag[:], in0=frac[:], scalar=-1.0, in1=frac[:], op0=ALU.mult, op1=ALU.max)
         warm = keep.tile([P, 1], F32, name="warm")
         nc.scalar.activation(out=warm[:], in_=pos[:, 0:1], func=ACT.Sin, scale=0.0)
 
         def tables():
-            nc.scalar.activation(out=mag[:], in_=frac[:], func=ACT.Abs)
             nc.scalar.activation(out=cos_t[:], in_=mag[:], func=ACT.Sin, scale=-2.0 * math.pi, bias=math.pi / 2.0)
             nc.scalar.activation(out=sin_t[:], in_=frac[:], func=ACT.Sin, scale=2.0 * math.pi)
 
@@ -150,6 +158,17 @@ def tile_attentionhead_pa_v_kernel(tc, x, W_qkv, sqk, q1, k1, grad_0, grad_1, gr
 
         staged = {}
 
+        def by_pe(out, in_):
+            for h in range(2):
+                tr = ps_t.tile([P, 256, J], BF16, tag="tr", name="itr")
+                for q in range(2):
+                    lo = h * 256 + q * P
+                    nc.tensor.matmul(
+                        tr[:, q * P : (q + 1) * P, :].rearrange("p c t -> p (c t)"), lhsT=ident_b[:],
+                        rhs=in_[:, :, lo : lo + P].rearrange("p t c -> p c t"), start=True, stop=True,
+                    )
+                nc.scalar.copy(out=out[:, h * 1024 : (h + 1) * 1024], in_=tr[:].rearrange("p c t -> p (c t)"))
+
         def stage_piece(copy, key):
             kind, a, n = key
             st = work.tile([P, J * D], BF16, tag="stage", name="stage", bufs=5, align_bytes=64)
@@ -161,7 +180,10 @@ def tile_attentionhead_pa_v_kernel(tc, x, W_qkv, sqk, q1, k1, grad_0, grad_1, gr
                 src = g2_t[n][:]
             else:
                 src = z_t[a][:]
-            interleave(copy, st[:], src)
+            if copy is None:
+                by_pe(st[:], src)
+            else:
+                interleave(copy, st[:], src)
             staged[key] = st
 
         def quant_piece(key):
@@ -206,7 +228,7 @@ def tile_attentionhead_pa_v_kernel(tc, x, W_qkv, sqk, q1, k1, grad_0, grad_1, gr
 
         def root(i):
             rt[i] = work.tile([P, 2], F32, tag="rt", name="rt", bufs=3)
-            nc.gpsimd.tensor_tensor(out=rt[i][:], in0=ss[i][:], in1=power[:], op=ALU.pow)
+            nc.scalar.activation(out=rt[i][:], in_=rr[i][:], func=ACT.Sqrt)
 
         def dot(i, jj):
             if jj == 0:
@@ -229,24 +251,25 @@ def tile_attentionhead_pa_v_kernel(tc, x, W_qkv, sqk, q1, k1, grad_0, grad_1, gr
                 op0=ALU.mult, op1=ALU.add,
             )
 
-        def times(i, jj, table, store, tag):
-            if jj == 0:
+        def times(i, jj, table, store, tag, lo=0, hi=H):
+            if jj == 0 and lo == 0:
                 store[i] = work.tile([P, 2, D], F32, tag=tag, name=tag)
             nc.vector.scalar_tensor_tensor(
-                out=store[i][:, jj, :].rearrange("p (h w) -> p h w", h=2),
-                in0=d_t[i][:, jj, :].rearrange("p (h w) -> p h w", h=2),
+                out=store[i][:, jj, :].rearrange("p (h w) -> p h w", h=2)[:, :, lo:hi],
+                in0=d_t[i][:, jj, :].rearrange("p (h w) -> p h w", h=2)[:, :, lo:hi],
                 scalar=rt[i][:, jj : jj + 1],
-                in1=table[:, 2 * (i % 2) + jj, :].unsqueeze(1).to_broadcast([P, 2, H]),
+                in1=table[:, 2 * (i % 2) + jj, lo:hi].unsqueeze(1).to_broadcast([P, 2, hi - lo]),
                 op0=ALU.mult, op1=ALU.mult,
             )
 
-        def rotate(i):
+        def rotate(i, lo=0, hi=H):
             if i % 2 == 0:
                 z_t[i // 2] = work.tile([P, J, D], BF16, tag="z", name="z", align_bytes=64)
             js = slice(2 * (i % 2), 2 * (i % 2) + 2)
             z, a, b = z_t[i // 2], a_t[i], b_t[i]
-            nc.vector.tensor_tensor(out=z[:, js, 0:H], in0=a[:, :, 0:H], in1=b[:, :, H:D], op=ALU.add)
-            nc.vector.tensor_tensor(out=z[:, js, H:D], in0=a[:, :, H:D], in1=b[:, :, 0:H], op=ALU.subtract)
+            one, two = slice(lo, hi), slice(H + lo, H + hi)
+            nc.vector.tensor_tensor(out=z[:, js, one], in0=a[:, :, one], in1=b[:, :, two], op=ALU.add)
+            nc.vector.tensor_tensor(out=z[:, js, two], in0=a[:, :, two], in1=b[:, :, one], op=ALU.subtract)
 
         fst = {}
 
@@ -326,27 +349,26 @@ def tile_attentionhead_pa_v_kernel(tc, x, W_qkv, sqk, q1, k1, grad_0, grad_1, gr
 
         sc, ve = nc.scalar.copy, nc.vector.tensor_copy
 
-        s_fill = {
-            0: [("x", 0, 0), ("x", 0, 1), ("v", 0, 0)],
-            1: [("x", 1, 0), ("x", 1, 1), ("v", 0, 1)],
-            2: [("w", 2, 0)],
-            3: [("w", 2, 1), ("w", 0, 0)],
-            4: [("w", 0, 1), ("w", 1, 0)],
-        }
-        v_fill = {
-            2: [("z", 0, 0)],
-            4: [("z", 1, 0)],
-            5: [("w", 1, 1)],
-            6: [("z", 2, 0)],
-        }
-        mx_plan = {
-            3: [("w", 2, 0), ("w", 2, 1)],
-            4: [("w", 2, 2), ("w", 2, 3)],
-            5: [("w", 0, 0), ("w", 0, 1)],
-            6: [("w", 0, 2), ("w", 0, 3), ("x", 0, 0), ("x", 0, 1)],
-            7: [("x", 0, 2), ("x", 0, 3), ("x", 1, 0)],
-            8: [("x", 1, 1)],
-        }
+        g_last = []
+
+        def window():
+            if g_last:
+                dst, lo, st, fmt = g_last.pop()
+                quantize(dst, lo, P, st[:], fmt)
+            if g_fill:
+                kind, a, n, sub = g_fill.pop(0)
+                src, dst = (x_t[a], x_q[a]) if kind == "x" else (w_t[a], w_q[a])
+                lo = n * D + sub * P
+                st = work.tile([P, J * P], BF16, tag="gs", name="gs", bufs=1, align_bytes=64)
+                nc.gpsimd.tensor_scalar(
+                    out=st[:].rearrange("p (c t) -> p c t", t=J),
+                    in0=src[:, :, lo : lo + P].rearrange("p t c -> p c t"),
+                    scalar1=1.0, scalar2=0.0, op0=ALU.mult, op1=ALU.add,
+                )
+                g_last.append((dst, lo, st, E4M3))
+
+        g_fill = [(kind, a, n, sub) for kind, a, n in PLAN["g"] for sub in range(4)]
+        s_fill, v_fill, mx_plan = PLAN["s"], PLAN["v"], PLAN["mx"]
         v_feats = {1: [("v", 0, 0), ("v", 0, 1)], 3: [("v", 1, 0), ("v", 1, 1)]}
 
         grad_transpose(0)
@@ -365,6 +387,7 @@ def tile_attentionhead_pa_v_kernel(tc, x, W_qkv, sqk, q1, k1, grad_0, grad_1, gr
         gain(1)
 
         pending = []
+        last = STEPS - 1
         for i in range(STEPS):
             nxt, pre = i + 1, i + 2
             if i > 0:
@@ -373,6 +396,7 @@ def tile_attentionhead_pa_v_kernel(tc, x, W_qkv, sqk, q1, k1, grad_0, grad_1, gr
                 grad_transpose(pre)
             for key in v_feats.get(i, []):
                 fea_transpose(key)
+            window()
             if nxt < STEPS:
                 dot(nxt, 0)
                 recip(nxt)
@@ -380,19 +404,19 @@ def tile_attentionhead_pa_v_kernel(tc, x, W_qkv, sqk, q1, k1, grad_0, grad_1, gr
                 dot(nxt, 1)
             if pre < STEPS:
                 squares(pre)
-            times(i, 0, cos_t, a_t, "A")
-            if nxt < STEPS:
+            for e, key in PLAN["e"].get(i, []):
+                stage_piece(sc if e == "s" else None, key)
+            if i < last:
+                times(i, 0, cos_t, a_t, "A")
                 alpha(nxt)
-            times(i, 1, cos_t, a_t, "A")
-            times(i, 0, sin_t, b_t, "B")
-            if nxt < STEPS:
+                times(i, 1, cos_t, a_t, "A")
+                times(i, 0, sin_t, b_t, "B")
+                times(i, 1, sin_t, b_t, "B")
+                window()
                 project(nxt, 0)
-            times(i, 1, sin_t, b_t, "B")
-            if nxt < STEPS:
                 project(nxt, 1)
-            if i < 7:
-                for item in mx_plan.get(i, []):
-                    do_mx(item, (sc, sc))
+            for item in mx_plan.get(i, []):
+                do_mx(item[:3], (sc, ve if item[3] else sc))
             if pre < STEPS:
                 gain(pre)
             for key in v_fill.get(i, []):
@@ -401,32 +425,49 @@ def tile_attentionhead_pa_v_kernel(tc, x, W_qkv, sqk, q1, k1, grad_0, grad_1, gr
                 fea_quant(i - 1)
             for key in v_feats.get(i, []):
                 fea_quant(key)
-            if i == 7:
-                for item in mx_plan.get(i, []):
-                    do_mx(item, (sc, sc))
-            rotate(i)
-            for key in pending + v_fill.get(i, []):
+            if i < last:
+                rotate(i)
+            for key in pending + [k for e, k in PLAN["e"].get(i, [])] + v_fill.get(i, []):
                 quant_piece(key)
-            pending = s_fill.get(i, [])
-            for key in pending:
-                stage_piece(sc, key)
+            pending = [k for e, k in s_fill.get(i, [])]
+            for e, key in s_fill.get(i, []):
+                stage_piece(sc if e == "s" else None, key)
+            for item in mx_plan.get(i + 0.5, []):
+                do_mx(item[:3], (sc, ve if item[3] else sc))
 
-        fea_transpose(STEPS - 1, ve)
-        for item in mx_plan[STEPS]:
-            do_mx(item, (sc, sc))
-        open_groups = [
-            (("x", 1, 2), mx_begin(("x", 1, 2), ps_mx, "mx")),
-            (("x", 1, 3), mx_begin(("x", 1, 3), ps_mx, "mx")),
-            (("w", 1, 0), mx_begin(("w", 1, 0), ps_h, "h")),
-        ]
+        open_groups = {}
+        for item, tag in PLAN["open"]:
+            open_groups[item] = mx_begin(item, ps_h if tag == "h" else ps_mx, tag)
         st = work.tile([P, J * D], BF16, tag="stage", name="stage", bufs=5, align_bytes=64)
-        for m in range(4):
-            cols = slice(m * P, (m + 1) * P)
-            interleave(ve if m < 3 else sc, st[:, m * D : (m + 1) * D], z_t[3][:, :, cols])
-        fea_quant(STEPS - 1)
-        for m in range(4):
+
+        def tail_stage(copy, m):
+            interleave(copy, st[:, m * D : (m + 1) * D], z_t[3][:, :, m * P : (m + 1) * P])
+
+        def tail_quant(m):
             quantize(tok_q[1][1], m * P, P, st[:, m * D : (m + 1) * D], E5M2)
-        for item, accs in open_groups:
-            mx_finish(item, accs, (sc, ve))
-        for m in range(1, 4):
-            do_mx(("w", 1, m), (sc, ve))
+
+        def half_times(lo, hi):
+            for jj in range(2):
+                times(last, jj, cos_t, a_t, "A", lo, hi)
+            for jj in range(2):
+                times(last, jj, sin_t, b_t, "B", lo, hi)
+
+        half_times(0, P)
+        half_times(P, H)
+        rotate(last, 0, P)
+        rotate(last, P, H)
+        tail_stage(ve, 0)
+        tail_stage(ve, 2)
+        fea_transpose(last, sc)
+        tail_stage(ve, 1)
+        tail_quant(0)
+        tail_quant(2)
+        tail_stage(sc, 3)
+        tail_quant(1)
+        fea_quant(last)
+        tail_quant(3)
+        for item in PLAN["finish"]:
+            if item in open_groups:
+                mx_finish(item, open_groups[item], (sc, ve))
+            else:
+                do_mx(item, (sc, ve))

@@ -24,22 +24,25 @@ FLOPS = 2 * 2 * (B * T) * (3 * D) * C
 UNITS = [(0, 0), (0, 1), (1, 0), (1, 1)]
 STEPS = 2 * len(UNITS)
 
-PLAN = {'e': {0: [('s', ('v', 0, 0))], 1: [('s', ('v', 0, 1))], 3: [('s', ('x', 1, 1))], 4: [('p', ('z', 0, 0))]},
+PLAN = {'e': {},
  'finish': [('w', 1, 0), ('w', 1, 2), ('w', 1, 1), ('x', 1, 3), ('x', 1, 2), ('w', 1, 3)],
- 'g': [('x', 0, 0), ('w', 0, 0), ('w', 1, 0)],
- 'mx': {3.5: [('w', 2, 0, 0)],
-        4.5: [('w', 2, 3, 0)],
-        5: [('w', 2, 2, 0), ('w', 2, 1, 0), ('w', 0, 3, 0)],
-        6.5: [('w', 0, 0, 0), ('w', 0, 1, 0), ('w', 0, 2, 0), ('x', 0, 1, 0), ('x', 0, 0, 0)],
-        7: [('x', 0, 3, 0)],
-        7.5: [('x', 1, 0, 1), ('x', 1, 1, 0), ('x', 0, 2, 0)]},
- 'open': [(('x', 1, 2), 'h'), (('w', 1, 0), 'mx'), (('w', 1, 2), 'mx')],
- 's': {0: [('p', ('x', 0, 1))],
-       1: [('p', ('x', 1, 0))],
-       2: [('s', ('w', 2, 1)), ('s', ('w', 2, 0))],
-       3: [('p', ('z', 1, 0))],
-       4: [('s', ('w', 1, 1)), ('p', ('w', 0, 1))]},
- 'v': {7: [('z', 2, 0)]}}
+ 'g': [('x', 0, 0), ('v', 0, 1), ('x', 1, 1), ('w', 2, 0), ('w', 1, 0), ('w', 0, 1)],
+ 'mx': {4.5: [('w', 2, 0, 1), ('w', 2, 1, 0)],
+        5: [('w', 0, 2, 0), ('w', 0, 1, 0)],
+        5.5: [('w', 2, 2, 0), ('w', 2, 3, 0), ('w', 0, 3, 0)],
+        6: [('x', 0, 1, 0)],
+        6.5: [('x', 0, 0, 0), ('x', 0, 2, 1)],
+        7: [('x', 0, 3, 0), ('w', 0, 0, 0)],
+        7.5: [('x', 1, 1, 0), ('x', 1, 0, 0)]},
+ 'open1': [],
+ 'open2': [(('x', 1, 2), 'h'), (('w', 1, 0), 'mx'), (('w', 1, 2), 'mx')],
+ 's': {0: [('s', ('x', 0, 1))],
+       1: [('s', ('x', 1, 0)), ('s', ('w', 2, 1))],
+       2: [('s', ('v', 0, 0)), ('s', ('w', 0, 0))],
+       3: [('s', ('z', 0, 0)), ('s', ('z', 1, 0))],
+       4: [('s', ('w', 1, 1))],
+       6: [('s', ('z', 2, 0))]},
+ 'v': {}}
 
 
 def tile_attentionhead_pa_v_kernel(tc, x, W_qkv, sqk, q1, k1, grad_0, grad_1, grad_2, out_0, out_1):
@@ -58,7 +61,7 @@ def tile_attentionhead_pa_v_kernel(tc, x, W_qkv, sqk, q1, k1, grad_0, grad_1, gr
         zrow = keep.tile([P, D], BF16, name="zrow")
         nc.vector.memset(zrow[:], 0.0)
         ones = keep.tile([P, P], BF16, name="ones")
-        nc.vector.memset(ones[:], 1.0)
+        nc.gpsimd.memset(ones[:], 1.0)
         pos = keep.tile([P, J], F32, name="pos")
         nc.gpsimd.iota(pos[:], [[1, J]], base=0, channel_multiplier=J, allow_small_or_imprecise_dtypes=True)
         ident_b = keep.tile([P, P], BF16, name="ident_b")
@@ -103,38 +106,55 @@ def tile_attentionhead_pa_v_kernel(tc, x, W_qkv, sqk, q1, k1, grad_0, grad_1, gr
         load_unit(3, 1)
         load_w(1)
 
-        freq = keep.tile([P, H], F32, name="freq")
-        nc.vector.tensor_scalar(out=freq[:, 0:1], in0=pos[:, 0:1], scalar1=0.0, scalar2=1.0 / (2.0 * math.pi), op0=ALU.mult, op1=ALU.add)
-        for k in range(8):
+        diag = keep.tile([P, 4, P], BF16, name="diag")
+        gain_ps = ps_h.tile([P, D], F32, tag="h", name="gain_ps")
+        nc.tensor.matmul(gain_ps[:], lhsT=ones[:], rhs=zrow[:], start=True, stop=True)
+
+        def gain_diag():
+            nc.vector.tensor_tensor(
+                out=diag[:],
+                in0=ident_b[:].unsqueeze(1).to_broadcast([P, 4, P]),
+                in1=gain_ps[:].rearrange("p (f n) -> p f n", f=4),
+                op=ALU.mult,
+            )
+
+        step16 = keep.tile([P, 2, 16], F32, name="step16")
+        for half, first in enumerate((1.0 / (2.0 * math.pi), 1.0)):
+            nc.vector.tensor_scalar(out=step16[:, half, 0:1], in0=pos[:, 0:1], scalar1=0.0, scalar2=first, op0=ALU.mult, op1=ALU.add)
+        for k in range(4):
             n = 1 << k
-            nc.vector.tensor_scalar_mul(freq[:, n : 2 * n], freq[:, 0:n], ROPE_BASE ** (-float(n) / H))
+            for half, unit in enumerate((1.0, 16.0)):
+                nc.vector.tensor_scalar_mul(step16[:, half, n : 2 * n], step16[:, half, 0:n], ROPE_BASE ** (-unit * n / H))
+        freq = keep.tile([P, H], F32, name="freq")
+        nc.vector.tensor_tensor(
+            out=freq[:].rearrange("p (a b) -> p a b", a=16),
+            in0=step16[:, 1, :].unsqueeze(2).to_broadcast([P, 16, 16]),
+            in1=step16[:, 0, :].unsqueeze(1).to_broadcast([P, 16, 16]),
+            op=ALU.mult,
+        )
         tau = work.tile([P, J, H], F32, tag="A", name="tau")
+        whole = work.tile([P, J, H], I32, tag="B", name="whole")
+        frac = work.tile([P, J, H], F32, tag="A", name="frac")
+        mag = work.tile([P, J, H], F32, tag="B", name="mag")
+        halves = [slice(0, 2), slice(2, 4)]
         for j in range(J):
             nc.vector.tensor_scalar_mul(tau[:, j, :], freq[:], pos[:, j : j + 1])
-        whole = work.tile([P, J, H], I32, tag="B", name="whole")
-        nc.vector.tensor_copy(out=whole[:], in_=tau[:])
-        frac = work.tile([P, J, H], F32, tag="A", name="frac")
-        nc.vector.tensor_tensor(out=frac[:], in0=tau[:], in1=whole[:], op=ALU.subtract)
+        gain_diag()
+        for js in halves:
+            nc.vector.tensor_copy(out=whole[:, js, :], in_=tau[:, js, :])
+        for js in halves:
+            nc.vector.tensor_tensor(out=frac[:, js, :], in0=tau[:, js, :], in1=whole[:, js, :], op=ALU.subtract)
+        for js in halves:
+            nc.vector.scalar_tensor_tensor(out=mag[:, js, :], in0=frac[:, js, :], scalar=-1.0, in1=frac[:, js, :], op0=ALU.mult, op1=ALU.max)
         sin_t = keep.tile([P, J, H], F32, name="sin_t")
         cos_t = keep.tile([P, J, H], F32, name="cos_t")
-        mag = work.tile([P, J, H], F32, tag="B", name="mag")
-        nc.vector.scalar_tensor_tensor(out=mag[:], in0=frac[:], scalar=-1.0, in1=frac[:], op0=ALU.mult, op1=ALU.max)
         warm = keep.tile([P, 1], F32, name="warm")
         nc.scalar.activation(out=warm[:], in_=pos[:, 0:1], func=ACT.Sin, scale=0.0)
 
-        def tables():
-            nc.scalar.activation(out=cos_t[:], in_=mag[:], func=ACT.Sin, scale=-2.0 * math.pi, bias=math.pi / 2.0)
-            nc.scalar.activation(out=sin_t[:], in_=frac[:], func=ACT.Sin, scale=2.0 * math.pi)
-
-        gain_ps = ps_h.tile([P, D], F32, tag="h", name="gain_ps")
-        nc.tensor.matmul(gain_ps[:], lhsT=ones[:], rhs=zrow[:], start=True, stop=True)
-        diag = keep.tile([P, 4, P], BF16, name="diag")
-        nc.vector.tensor_tensor(
-            out=diag[:],
-            in0=ident_b[:].unsqueeze(1).to_broadcast([P, 4, P]),
-            in1=gain_ps[:].rearrange("p (f n) -> p f n", f=4),
-            op=ALU.mult,
-        )
+        def tables(h):
+            js = halves[h]
+            nc.scalar.activation(out=cos_t[:, js, :], in_=mag[:, js, :], func=ACT.Sin, scale=-2.0 * math.pi, bias=math.pi / 2.0)
+            nc.scalar.activation(out=sin_t[:, js, :], in_=frac[:, js, :], func=ACT.Sin, scale=2.0 * math.pi)
 
         def codes(tag, width):
             c = keep.tile([P, width], U32, name=tag + "_c", align_bytes=64)
@@ -169,17 +189,17 @@ def tile_attentionhead_pa_v_kernel(tc, x, W_qkv, sqk, q1, k1, grad_0, grad_1, gr
                     )
                 nc.scalar.copy(out=out[:, h * 1024 : (h + 1) * 1024], in_=tr[:].rearrange("p c t -> p (c t)"))
 
-        def stage_piece(copy, key):
+        def source(key):
             kind, a, n = key
-            st = work.tile([P, J * D], BF16, tag="stage", name="stage", bufs=5, align_bytes=64)
             if kind == "x":
-                src = x_t[a][:, :, n * D : (n + 1) * D]
-            elif kind == "w":
-                src = w_t[a][:, :, n * D : (n + 1) * D]
-            elif kind == "v":
-                src = g2_t[n][:]
-            else:
-                src = z_t[a][:]
+                return x_t[a][:, :, n * D : (n + 1) * D]
+            if kind == "w":
+                return w_t[a][:, :, n * D : (n + 1) * D]
+            return g2_t[n][:] if kind == "v" else z_t[a][:]
+
+        def stage_piece(copy, key):
+            st = work.tile([P, J * D], BF16, tag="stage", name="stage", bufs=4, align_bytes=64)
+            src = source(key)
             if copy is None:
                 by_pe(st[:], src)
             else:
@@ -201,13 +221,18 @@ def tile_attentionhead_pa_v_kernel(tc, x, W_qkv, sqk, q1, k1, grad_0, grad_1, gr
 
         z_t, gT, h_t, ss, rr, rt, dots, nal, d_t, a_t, b_t = {}, {}, {}, {}, {}, {}, {}, {}, {}, {}, {}
 
-        def grad_transpose(i, copy=nc.scalar.copy):
+        gtr = {}
+
+        def grad_transpose(i):
             tr = ps_t.tile([P, 2, 4, P], BF16, tag="tr", name="gtr")
             for jj in range(2):
                 for f in range(4):
                     nc.tensor.transpose(tr[:, jj, f, :], g_t[i // 2][:, 2 * (i % 2) + jj, f * P : (f + 1) * P], ident_b[:])
+            gtr[i] = tr
+
+        def grad_copy(i, copy):
             gT[i] = work.tile([P, 2, 4, P], BF16, tag="gT", name="gT", bufs=2)
-            copy(out=gT[i][:], in_=tr[:])
+            copy(out=gT[i][:], in_=gtr[i][:])
 
         def gain(i):
             for jj in range(2):
@@ -241,7 +266,9 @@ def tile_attentionhead_pa_v_kernel(tc, x, W_qkv, sqk, q1, k1, grad_0, grad_1, gr
 
         def alpha(i):
             nal[i] = work.tile([P, 2], F32, tag="nal", name="nal", bufs=3)
-            nc.vector.scalar_tensor_tensor(out=nal[i][:], in0=dots[i][:], scalar=-1.0, in1=rr[i][:], op0=ALU.mult, op1=ALU.mult)
+            for jj in range(2):
+                col = slice(jj, jj + 1)
+                nc.vector.tensor_scalar(out=nal[i][:, col], in0=dots[i][:, col], scalar1=rr[i][:, col], scalar2=-1.0, op0=ALU.mult, op1=ALU.mult)
 
         def project(i, jj):
             if jj == 0:
@@ -262,13 +289,14 @@ def tile_attentionhead_pa_v_kernel(tc, x, W_qkv, sqk, q1, k1, grad_0, grad_1, gr
                 op0=ALU.mult, op1=ALU.mult,
             )
 
-        def rotate(i, lo=0, hi=H):
+        def rotate(i, between, lo=0, hi=H):
             if i % 2 == 0:
                 z_t[i // 2] = work.tile([P, J, D], BF16, tag="z", name="z", align_bytes=64)
             js = slice(2 * (i % 2), 2 * (i % 2) + 2)
             z, a, b = z_t[i // 2], a_t[i], b_t[i]
             one, two = slice(lo, hi), slice(H + lo, H + hi)
             nc.vector.tensor_tensor(out=z[:, js, one], in0=a[:, :, one], in1=b[:, :, two], op=ALU.add)
+            between()
             nc.vector.tensor_tensor(out=z[:, js, two], in0=a[:, :, two], in1=b[:, :, one], op=ALU.subtract)
 
         fst = {}
@@ -353,70 +381,71 @@ def tile_attentionhead_pa_v_kernel(tc, x, W_qkv, sqk, q1, k1, grad_0, grad_1, gr
 
         def window():
             if g_last:
-                dst, lo, st, fmt = g_last.pop()
-                quantize(dst, lo, P, st[:], fmt)
+                quant_piece(g_last.pop())
             if g_fill:
-                kind, a, n, sub = g_fill.pop(0)
-                src, dst = (x_t[a], x_q[a]) if kind == "x" else (w_t[a], w_q[a])
-                lo = n * D + sub * P
-                st = work.tile([P, J * P], BF16, tag="gs", name="gs", bufs=1, align_bytes=64)
+                key = g_fill.pop(0)
+                st = work.tile([P, J * D], BF16, tag="gs", name="gs", bufs=1, align_bytes=64)
                 nc.gpsimd.tensor_scalar(
                     out=st[:].rearrange("p (c t) -> p c t", t=J),
-                    in0=src[:, :, lo : lo + P].rearrange("p t c -> p c t"),
+                    in0=source(key).rearrange("p t c -> p c t"),
                     scalar1=1.0, scalar2=0.0, op0=ALU.mult, op1=ALU.add,
                 )
-                g_last.append((dst, lo, st, E4M3))
+                staged[key] = st
+                g_last.append(key)
 
-        g_fill = [(kind, a, n, sub) for kind, a, n in PLAN["g"] for sub in range(4)]
+        g_fill = list(PLAN["g"])
         s_fill, v_fill, mx_plan = PLAN["s"], PLAN["v"], PLAN["mx"]
         v_feats = {1: [("v", 0, 0), ("v", 0, 1)], 3: [("v", 1, 0), ("v", 1, 1)]}
 
+        last = STEPS - 1
         grad_transpose(0)
-        grad_transpose(1, nc.vector.tensor_copy)
+        grad_copy(0, sc)
+        grad_transpose(1)
         squares(0)
         gain(0)
+        tables(0)
         dot(0, 0)
         dot(0, 1)
         recip(0)
-        tables()
-        squares(1)
+        grad_copy(1, ve)
         alpha(0)
         project(0, 0)
         project(0, 1)
-        root(0)
         gain(1)
+        squares(1)
+        tables(1)
+        root(0)
+        recip(1)
+        root(1)
 
         pending = []
-        last = STEPS - 1
-        for i in range(STEPS):
+        window()
+        for i in range(last):
             nxt, pre = i + 1, i + 2
             if i > 0:
                 fea_transpose(i - 1)
             if pre < STEPS:
                 grad_transpose(pre)
+                grad_copy(pre, sc)
             for key in v_feats.get(i, []):
                 fea_transpose(key)
-            window()
-            if nxt < STEPS:
-                dot(nxt, 0)
-                recip(nxt)
+            if i > 0:
                 root(nxt)
-                dot(nxt, 1)
+            dot(nxt, 0)
+            dot(nxt, 1)
             if pre < STEPS:
                 squares(pre)
+            alpha(nxt)
+            project(nxt, 0)
+            project(nxt, 1)
             for e, key in PLAN["e"].get(i, []):
                 stage_piece(sc if e == "s" else None, key)
-            if i < last:
-                times(i, 0, cos_t, a_t, "A")
-                alpha(nxt)
-                times(i, 1, cos_t, a_t, "A")
-                times(i, 0, sin_t, b_t, "B")
-                times(i, 1, sin_t, b_t, "B")
-                window()
-                project(nxt, 0)
-                project(nxt, 1)
             for item in mx_plan.get(i, []):
                 do_mx(item[:3], (sc, ve if item[3] else sc))
+            for jj in range(2):
+                times(i, jj, cos_t, a_t, "A")
+            for jj in range(2):
+                times(i, jj, sin_t, b_t, "B")
             if pre < STEPS:
                 gain(pre)
             for key in v_fill.get(i, []):
@@ -425,20 +454,31 @@ def tile_attentionhead_pa_v_kernel(tc, x, W_qkv, sqk, q1, k1, grad_0, grad_1, gr
                 fea_quant(i - 1)
             for key in v_feats.get(i, []):
                 fea_quant(key)
-            if i < last:
-                rotate(i)
+            if pre < STEPS:
+                recip(pre)
             for key in pending + [k for e, k in PLAN["e"].get(i, [])] + v_fill.get(i, []):
                 quant_piece(key)
+            rotate(i, window)
             pending = [k for e, k in s_fill.get(i, [])]
             for e, key in s_fill.get(i, []):
                 stage_piece(sc if e == "s" else None, key)
             for item in mx_plan.get(i + 0.5, []):
                 do_mx(item[:3], (sc, ve if item[3] else sc))
 
-        open_groups = {}
-        for item, tag in PLAN["open"]:
-            open_groups[item] = mx_begin(item, ps_h if tag == "h" else ps_mx, tag)
-        st = work.tile([P, J * D], BF16, tag="stage", name="stage", bufs=5, align_bytes=64)
+        fea_transpose(last - 1)
+        while g_last:
+            quant_piece(g_last.pop())
+        for e, key in PLAN["e"].get(last, []):
+            stage_piece(sc if e == "s" else None, key)
+        fea_quant(last - 1)
+        for key in v_fill.get(last, []):
+            stage_piece(ve, key)
+        for key in pending + [k for e, k in PLAN["e"].get(last, [])] + v_fill.get(last, []):
+            quant_piece(key)
+        for item in mx_plan.get(last, []):
+            do_mx(item[:3], (sc, ve if item[3] else sc))
+
+        st = work.tile([P, J * D], BF16, tag="stage", name="stage", bufs=4, align_bytes=64)
 
         def tail_stage(copy, m):
             interleave(copy, st[:, m * D : (m + 1) * D], z_t[3][:, :, m * P : (m + 1) * P])
@@ -454,11 +494,18 @@ def tile_attentionhead_pa_v_kernel(tc, x, W_qkv, sqk, q1, k1, grad_0, grad_1, gr
 
         half_times(0, P)
         half_times(P, H)
-        rotate(last, 0, P)
-        rotate(last, P, H)
+        rotate(last, lambda: None, 0, P)
+        rotate(last, lambda: None, P, H)
+        for item in mx_plan.get(last + 0.5, []):
+            do_mx(item[:3], (sc, ve if item[3] else sc))
+        open_groups = {}
+        for item, tag in PLAN["open1"]:
+            open_groups[item] = mx_begin(item, ps_h if tag == "h" else ps_mx, tag)
         tail_stage(ve, 0)
         tail_stage(ve, 2)
         fea_transpose(last, sc)
+        for item, tag in PLAN["open2"]:
+            open_groups[item] = mx_begin(item, ps_h if tag == "h" else ps_mx, tag)
         tail_stage(ve, 1)
         tail_quant(0)
         tail_quant(2)

@@ -21,28 +21,31 @@ H = D // 2
 ROPE_BASE = 10000.0
 FLOPS = 2 * 2 * (B * T) * (3 * D) * C
 
-UNITS = [(0, 0), (0, 1), (1, 0), (1, 1)]
+UNITS = [(0, 0), (1, 0), (0, 1), (1, 1)]
 STEPS = 2 * len(UNITS)
 
 PLAN = {'e': {},
- 'finish': [('w', 1, 0), ('w', 1, 2), ('w', 1, 1), ('x', 1, 3), ('x', 1, 2), ('w', 1, 3)],
- 'g': [('x', 0, 0), ('v', 0, 1), ('x', 1, 1), ('w', 2, 0), ('w', 1, 0), ('w', 0, 1)],
- 'mx': {4.5: [('w', 2, 0, 1), ('w', 2, 1, 0)],
-        5: [('w', 0, 2, 0), ('w', 0, 1, 0)],
-        5.5: [('w', 2, 2, 0), ('w', 2, 3, 0), ('w', 0, 3, 0)],
-        6: [('x', 0, 1, 0)],
-        6.5: [('x', 0, 0, 0), ('x', 0, 2, 1)],
-        7: [('x', 0, 3, 0), ('w', 0, 0, 0)],
-        7.5: [('x', 1, 1, 0), ('x', 1, 0, 0)]},
+ 'finish': [('w', 1, 0), ('w', 1, 1), ('w', 1, 3), ('x', 1, 3), ('w', 1, 2), ('x', 1, 2)],
+ 'g': [('w', 2, 1), ('w', 0, 0), ('x', 0, 1), ('w', 1, 1), ('x', 0, 0), ('z', 1, 0), ('z', 2, 0)],
+ 'gt': 0,
+ 'mx': {3.5: [('x', 0, 1, 0)],
+        5: [('x', 0, 0, 0)],
+        5.5: [('x', 0, 2, 0), ('w', 2, 2, 0)],
+        6: [('x', 0, 3, 0)],
+        6.5: [('w', 2, 3, 0), ('w', 2, 0, 0), ('w', 2, 1, 0)],
+        7: [('w', 0, 0, 1), ('w', 0, 2, 1), ('x', 1, 1, 0), ('x', 1, 0, 0)],
+        7.5: [('w', 0, 3, 0), ('w', 0, 1, 0)]},
  'open1': [],
- 'open2': [(('x', 1, 2), 'h'), (('w', 1, 0), 'mx'), (('w', 1, 2), 'mx')],
- 's': {0: [('s', ('x', 0, 1))],
-       1: [('s', ('x', 1, 0)), ('s', ('w', 2, 1))],
-       2: [('s', ('v', 0, 0)), ('s', ('w', 0, 0))],
-       3: [('s', ('z', 0, 0)), ('s', ('z', 1, 0))],
-       4: [('s', ('w', 1, 1))],
-       6: [('s', ('z', 2, 0))]},
- 'v': {}}
+ 'open2': [(('w', 1, 0), 'h')],
+ 's': {0: [('s', ('w', 2, 0))],
+       1: [('s', ('w', 0, 1)), ('s', ('z', 0, 0))],
+       2: [('s', ('w', 1, 0)), ('s', ('v', 0, 1))],
+       3: [('s', ('v', 0, 0))],
+       4: [('s', ('x', 1, 0)), ('s', ('x', 1, 1))]},
+ 'tags': ['h', 'tr', 'h', 'tr', 'mx', 'h'],
+ 'ts': 0,
+ 'v': {},
+ 'z6': 1}
 
 
 def tile_attentionhead_pa_v_kernel(tc, x, W_qkv, sqk, q1, k1, grad_0, grad_1, grad_2, out_0, out_1):
@@ -55,7 +58,8 @@ def tile_attentionhead_pa_v_kernel(tc, x, W_qkv, sqk, q1, k1, grad_0, grad_1, gr
         work = ctx.enter_context(tc.tile_pool(name="work", bufs=2))
         ps_h = ctx.enter_context(tc.psum_pool(name="ps_h", bufs=2))
         ps_t = ctx.enter_context(tc.psum_pool(name="ps_t", bufs=2))
-        ps_mx = ctx.enter_context(tc.psum_pool(name="ps_mx", bufs=4))
+        ps_mx = ctx.enter_context(tc.psum_pool(name="ps_mx", bufs=2))
+        ps_c = ctx.enter_context(tc.psum_pool(name="ps_c", bufs=1))
         ctx.enter_context(tc.manual_schedule())
 
         zrow = keep.tile([P, D], BF16, name="zrow")
@@ -86,25 +90,25 @@ def tile_attentionhead_pa_v_kernel(tc, x, W_qkv, sqk, q1, k1, grad_0, grad_1, gr
             nc.sync.dma_start(out=g2_t[b][:], in_=grad_2[b].rearrange("(p j) w -> p j w", j=J))
 
         def load_x(b):
-            x_t[b] = work.tile([P, J, C], BF16, tag="x", name="x_in", bufs=2)
+            x_t[b] = work.tile([P, J, C], BF16, tag="xw", name="x_in", bufs=4)
             nc.sync.dma_start(out=x_t[b][:], in_=x[b].rearrange("(p j) c -> p j c", j=J))
 
         def load_w(s):
-            w_t[s] = work.tile([P, J, C], BF16, tag="w", name="w_in", bufs=2)
+            w_t[s] = work.tile([P, J, C], BF16, tag="xw", name="w_in", bufs=4)
             nc.sync.dma_start(out=w_t[s][:], in_=W_qkv[s * D : (s + 1) * D, :].rearrange("(p j) c -> p j c", j=J))
 
         nc.sync.dma_start(out=zrow[0:1, :], in_=sqk.rearrange("(o n) -> o n", o=1))
         load_unit(0, 2)
-        load_x(0)
-        load_unit(1, 1)
-        load_g2(0)
-        load_x(1)
-        load_g2(1)
         load_w(2)
-        load_unit(2, 1)
+        load_unit(1, 1)
         load_w(0)
-        load_unit(3, 1)
+        load_g2(0)
         load_w(1)
+        load_unit(2, 1)
+        load_x(0)
+        load_g2(1)
+        load_x(1)
+        load_unit(3, 1)
 
         diag = keep.tile([P, 4, P], BF16, name="diag")
         gain_ps = ps_h.tile([P, D], F32, tag="h", name="gain_ps")
@@ -139,22 +143,36 @@ def tile_attentionhead_pa_v_kernel(tc, x, W_qkv, sqk, q1, k1, grad_0, grad_1, gr
         halves = [slice(0, 2), slice(2, 4)]
         for j in range(J):
             nc.vector.tensor_scalar_mul(tau[:, j, :], freq[:], pos[:, j : j + 1])
-        gain_diag()
         for js in halves:
             nc.vector.tensor_copy(out=whole[:, js, :], in_=tau[:, js, :])
-        for js in halves:
+        def reduce_angle(h):
+            js = halves[h]
             nc.vector.tensor_tensor(out=frac[:, js, :], in0=tau[:, js, :], in1=whole[:, js, :], op=ALU.subtract)
-        for js in halves:
+
+        def magnitude(h):
+            js = halves[h]
             nc.vector.scalar_tensor_tensor(out=mag[:, js, :], in0=frac[:, js, :], scalar=-1.0, in1=frac[:, js, :], op0=ALU.mult, op1=ALU.max)
+
+        reduce_angle(0)
+        gain_diag()
+        magnitude(0)
+        reduce_angle(1)
         sin_t = keep.tile([P, J, H], F32, name="sin_t")
         cos_t = keep.tile([P, J, H], F32, name="cos_t")
         warm = keep.tile([P, 1], F32, name="warm")
         nc.scalar.activation(out=warm[:], in_=pos[:, 0:1], func=ACT.Sin, scale=0.0)
 
+        cos_ps = []
+
         def tables(h):
             js = halves[h]
             nc.scalar.activation(out=cos_t[:, js, :], in_=mag[:, js, :], func=ACT.Sin, scale=-2.0 * math.pi, bias=math.pi / 2.0)
             nc.scalar.activation(out=sin_t[:, js, :], in_=frac[:, js, :], func=ACT.Sin, scale=2.0 * math.pi)
+            cos_ps.append(ps_c.tile([P, 2, H], F32, tag="cos%d" % h, name="cos_ps"))
+            nc.tensor.matmul(
+                cos_ps[h][:].rearrange("p j w -> p (j w)"), lhsT=ident_f[:],
+                rhs=cos_t[:, js, :].rearrange("p j w -> p (j w)"), start=True, stop=True,
+            )
 
         def codes(tag, width):
             c = keep.tile([P, width], U32, name=tag + "_c", align_bytes=64)
@@ -223,16 +241,21 @@ def tile_attentionhead_pa_v_kernel(tc, x, W_qkv, sqk, q1, k1, grad_0, grad_1, gr
 
         gtr = {}
 
-        def grad_transpose(i):
-            tr = ps_t.tile([P, 2, 4, P], BF16, tag="tr", name="gtr")
-            for jj in range(2):
-                for f in range(4):
-                    nc.tensor.transpose(tr[:, jj, f, :], g_t[i // 2][:, 2 * (i % 2) + jj, f * P : (f + 1) * P], ident_b[:])
-            gtr[i] = tr
+        def grad_transpose(i, parts=1):
+            gtr[i] = []
+            for q in range(parts):
+                tr = ps_t.tile([P, 2 // parts, 4, P], BF16, tag="tr", name="gtr")
+                for jj in range(2 // parts):
+                    for f in range(4):
+                        j = 2 * (i % 2) + 2 * q // parts + jj
+                        nc.tensor.transpose(tr[:, jj, f, :], g_t[i // 2][:, j, f * P : (f + 1) * P], ident_b[:])
+                gtr[i].append(tr)
 
         def grad_copy(i, copy):
             gT[i] = work.tile([P, 2, 4, P], BF16, tag="gT", name="gT", bufs=2)
-            copy(out=gT[i][:], in_=gtr[i][:])
+            n = 2 // len(gtr[i])
+            for q, tr in enumerate(gtr[i]):
+                copy(out=gT[i][:, q * n : (q + 1) * n, :, :], in_=tr[:])
 
         def gain(i):
             for jj in range(2):
@@ -285,18 +308,17 @@ def tile_attentionhead_pa_v_kernel(tc, x, W_qkv, sqk, q1, k1, grad_0, grad_1, gr
                 out=store[i][:, jj, :].rearrange("p (h w) -> p h w", h=2)[:, :, lo:hi],
                 in0=d_t[i][:, jj, :].rearrange("p (h w) -> p h w", h=2)[:, :, lo:hi],
                 scalar=rt[i][:, jj : jj + 1],
-                in1=table[:, 2 * (i % 2) + jj, lo:hi].unsqueeze(1).to_broadcast([P, 2, hi - lo]),
+                in1=table[:, jj, lo:hi].unsqueeze(1).to_broadcast([P, 2, hi - lo]),
                 op0=ALU.mult, op1=ALU.mult,
             )
 
-        def rotate(i, between, lo=0, hi=H):
+        def rotate(i, lo=0, hi=H):
             if i % 2 == 0:
                 z_t[i // 2] = work.tile([P, J, D], BF16, tag="z", name="z", align_bytes=64)
             js = slice(2 * (i % 2), 2 * (i % 2) + 2)
             z, a, b = z_t[i // 2], a_t[i], b_t[i]
             one, two = slice(lo, hi), slice(H + lo, H + hi)
             nc.vector.tensor_tensor(out=z[:, js, one], in0=a[:, :, one], in1=b[:, :, two], op=ALU.add)
-            between()
             nc.vector.tensor_tensor(out=z[:, js, two], in0=a[:, :, two], in1=b[:, :, one], op=ALU.subtract)
 
         fst = {}
@@ -339,7 +361,10 @@ def tile_attentionhead_pa_v_kernel(tc, x, W_qkv, sqk, q1, k1, grad_0, grad_1, gr
                         stop=(k == count - 1),
                     )
 
-        def accs_of(pool, tag):
+        pools = {"h": ps_h, "mx": ps_mx, "tr": ps_t}
+
+        def accs_of(tag):
+            pool = pools[tag]
             a0 = pool.tile([P, D], F32, tag=tag, name="acc0")
             a1 = pool.tile([P, D], F32, tag=tag, name="acc1")
             return a0, a1
@@ -348,7 +373,12 @@ def tile_attentionhead_pa_v_kernel(tc, x, W_qkv, sqk, q1, k1, grad_0, grad_1, gr
             o = work.tile([P, C], F32, tag="o", name="o", bufs=5)
             for n in range(2):
                 engines[n](out=o[:, n * D : (n + 1) * D], in_=accs[n][:])
-            nc.sync.dma_start(out=dest, in_=o[:])
+                if halves_out:
+                    nc.sync.dma_start(out=dest[:, n * D : (n + 1) * D], in_=o[:, n * D : (n + 1) * D])
+            if not halves_out:
+                nc.sync.dma_start(out=dest, in_=o[:])
+
+        halves_out = []
 
         def operands(item):
             kind, a, n = item
@@ -358,9 +388,9 @@ def tile_attentionhead_pa_v_kernel(tc, x, W_qkv, sqk, q1, k1, grad_0, grad_1, gr
             view = out_0[a].rearrange("(p j) c -> p j c", j=J)
             return [fea_q[s][a] for s in (2, 0, 1)], [w_q[s] for s in (2, 0, 1)], n * P, view[:, n, :]
 
-        def mx_begin(item, pool, tag):
+        def mx_begin(item, tag):
             lhs, rhs, lo, dest = operands(item)
-            accs = accs_of(pool, tag)
+            accs = accs_of(tag)
             passes(accs, lhs, rhs, lo, range(len(lhs) - 1), len(lhs))
             return accs
 
@@ -369,9 +399,9 @@ def tile_attentionhead_pa_v_kernel(tc, x, W_qkv, sqk, q1, k1, grad_0, grad_1, gr
             passes(accs, lhs, rhs, lo, [len(lhs) - 1], len(lhs))
             empty(accs, dest, engines)
 
-        def do_mx(item, engines):
+        def do_mx(item, engines, tag="mx"):
             lhs, rhs, lo, dest = operands(item)
-            accs = accs_of(ps_mx, "mx")
+            accs = accs_of(tag)
             passes(accs, lhs, rhs, lo, range(len(lhs)), len(lhs))
             empty(accs, dest, engines)
 
@@ -395,20 +425,21 @@ def tile_attentionhead_pa_v_kernel(tc, x, W_qkv, sqk, q1, k1, grad_0, grad_1, gr
 
         g_fill = list(PLAN["g"])
         s_fill, v_fill, mx_plan = PLAN["s"], PLAN["v"], PLAN["mx"]
-        v_feats = {1: [("v", 0, 0), ("v", 0, 1)], 3: [("v", 1, 0), ("v", 1, 1)]}
+        v_feats = {1: [("v", 0, 0), ("v", 0, 1)], 4: [("v", 1, 0), ("v", 1, 1)]}
 
         last = STEPS - 1
-        grad_transpose(0)
+        grad_transpose(0, 2)
         grad_copy(0, sc)
+        gain(0)
         grad_transpose(1)
         squares(0)
-        gain(0)
         tables(0)
         dot(0, 0)
         dot(0, 1)
         recip(0)
-        grad_copy(1, ve)
+        magnitude(1)
         alpha(0)
+        grad_copy(1, ve)
         project(0, 0)
         project(0, 1)
         gain(1)
@@ -426,13 +457,16 @@ def tile_attentionhead_pa_v_kernel(tc, x, W_qkv, sqk, q1, k1, grad_0, grad_1, gr
                 fea_transpose(i - 1)
             if pre < STEPS:
                 grad_transpose(pre)
-                grad_copy(pre, sc)
+                if not PLAN["gt"]:
+                    grad_copy(pre, sc)
             for key in v_feats.get(i, []):
                 fea_transpose(key)
             if i > 0:
                 root(nxt)
             dot(nxt, 0)
             dot(nxt, 1)
+            if pre < STEPS and PLAN["gt"]:
+                grad_copy(pre, ve)
             if pre < STEPS:
                 squares(pre)
             alpha(nxt)
@@ -443,9 +477,9 @@ def tile_attentionhead_pa_v_kernel(tc, x, W_qkv, sqk, q1, k1, grad_0, grad_1, gr
             for item in mx_plan.get(i, []):
                 do_mx(item[:3], (sc, ve if item[3] else sc))
             for jj in range(2):
-                times(i, jj, cos_t, a_t, "A")
+                times(i, jj, cos_ps[i % 2], a_t, "A")
             for jj in range(2):
-                times(i, jj, sin_t, b_t, "B")
+                times(i, jj, sin_t[:, 2 * (i % 2) : 2 * (i % 2) + 2, :], b_t, "B")
             if pre < STEPS:
                 gain(pre)
             for key in v_fill.get(i, []):
@@ -458,26 +492,23 @@ def tile_attentionhead_pa_v_kernel(tc, x, W_qkv, sqk, q1, k1, grad_0, grad_1, gr
                 recip(pre)
             for key in pending + [k for e, k in PLAN["e"].get(i, [])] + v_fill.get(i, []):
                 quant_piece(key)
-            rotate(i, window)
+            rotate(i)
+            window()
             pending = [k for e, k in s_fill.get(i, [])]
             for e, key in s_fill.get(i, []):
                 stage_piece(sc if e == "s" else None, key)
-            for item in mx_plan.get(i + 0.5, []):
-                do_mx(item[:3], (sc, ve if item[3] else sc))
+            for n, item in enumerate(mx_plan.get(i + 0.5, [])):
+                do_mx(item[:3], (sc, ve if item[3] else sc), "h" if i == last - 1 and n % 2 == 0 else "mx")
 
-        fea_transpose(last - 1)
+        fea_transpose(last - 1, sc if PLAN["z6"] else ve)
         while g_last:
             quant_piece(g_last.pop())
         for e, key in PLAN["e"].get(last, []):
             stage_piece(sc if e == "s" else None, key)
-        fea_quant(last - 1)
         for key in v_fill.get(last, []):
             stage_piece(ve, key)
         for key in pending + [k for e, k in PLAN["e"].get(last, [])] + v_fill.get(last, []):
             quant_piece(key)
-        for item in mx_plan.get(last, []):
-            do_mx(item[:3], (sc, ve if item[3] else sc))
-
         st = work.tile([P, J * D], BF16, tag="stage", name="stage", bufs=4, align_bytes=64)
 
         def tail_stage(copy, m):
@@ -488,33 +519,40 @@ def tile_attentionhead_pa_v_kernel(tc, x, W_qkv, sqk, q1, k1, grad_0, grad_1, gr
 
         def half_times(lo, hi):
             for jj in range(2):
-                times(last, jj, cos_t, a_t, "A", lo, hi)
+                times(last, jj, cos_ps[last % 2], a_t, "A", lo, hi)
             for jj in range(2):
-                times(last, jj, sin_t, b_t, "B", lo, hi)
+                times(last, jj, sin_t[:, 2 * (last % 2) : 2 * (last % 2) + 2, :], b_t, "B", lo, hi)
 
         half_times(0, P)
+        fea_quant(last - 1)
+        for n, item in enumerate(mx_plan.get(last, [])):
+            do_mx(item[:3], (sc, ve if item[3] else sc), ("h", "mx")[n % 2])
         half_times(P, H)
-        rotate(last, lambda: None, 0, P)
-        rotate(last, lambda: None, P, H)
-        for item in mx_plan.get(last + 0.5, []):
-            do_mx(item[:3], (sc, ve if item[3] else sc))
+        rotate(last, 0, P)
+        rotate(last, P, H)
+        for n, item in enumerate(mx_plan.get(last + 0.5, [])):
+            do_mx(item[:3], (sc, ve if item[3] else sc), ("h", "mx")[n % 2])
         open_groups = {}
         for item, tag in PLAN["open1"]:
-            open_groups[item] = mx_begin(item, ps_h if tag == "h" else ps_mx, tag)
+            open_groups[item] = mx_begin(item, tag)
         tail_stage(ve, 0)
         tail_stage(ve, 2)
         fea_transpose(last, sc)
+        for item in mx_plan.get(last + 1, []):
+            do_mx(item[:3], (sc, ve if item[3] else sc), "h")
         for item, tag in PLAN["open2"]:
-            open_groups[item] = mx_begin(item, ps_h if tag == "h" else ps_mx, tag)
+            open_groups[item] = mx_begin(item, tag)
         tail_stage(ve, 1)
         tail_quant(0)
         tail_quant(2)
-        tail_stage(sc, 3)
+        tail_stage(sc if PLAN["ts"] else ve, 3)
         tail_quant(1)
         fea_quant(last)
         tail_quant(3)
-        for item in PLAN["finish"]:
+        for n, item in enumerate(PLAN["finish"]):
+            if n == 4:
+                halves_out.append(1)
             if item in open_groups:
                 mx_finish(item, open_groups[item], (sc, ve))
             else:
-                do_mx(item, (sc, ve))
+                do_mx(item, (sc, ve), PLAN["tags"][n])

@@ -19,55 +19,63 @@ J = 4
 B, T, C, D = 2, 512, 1024, 512
 H = D // 2
 ROPE_BASE = 10000.0
+Q, K, V = 0, 1, 2
 FLOPS = 2 * 2 * (B * T) * (3 * D) * C
 
-UNITS = [(0, 0), (1, 0), (0, 1), (1, 1)]
+UNITS = [(Q, 0), (K, 0), (Q, 1), (K, 1)]
 STEPS = 2 * len(UNITS)
+LAST = STEPS - 1
 
-PLAN = {'e': {},
- 'finish': [('w', 1, 0), ('w', 1, 1), ('w', 1, 3), ('x', 1, 3), ('w', 1, 2), ('x', 1, 2)],
- 'g': [('w', 2, 1), ('w', 0, 0), ('x', 0, 1), ('w', 1, 1), ('x', 0, 0), ('z', 1, 0), ('z', 2, 0)],
- 'gt': 0,
- 'mx': {3.5: [('x', 0, 1, 0)],
-        5: [('x', 0, 0, 0)],
-        5.5: [('x', 0, 2, 0), ('w', 2, 2, 0)],
-        6: [('x', 0, 3, 0)],
-        6.5: [('w', 2, 3, 0), ('w', 2, 0, 0), ('w', 2, 1, 0)],
-        7: [('w', 0, 0, 1), ('w', 0, 2, 1), ('x', 1, 1, 0), ('x', 1, 0, 0)],
-        7.5: [('w', 0, 3, 0), ('w', 0, 1, 0)]},
- 'open1': [],
- 'open2': [(('w', 1, 0), 'h')],
- 's': {0: [('s', ('w', 2, 0))],
-       1: [('s', ('w', 0, 1)), ('s', ('z', 0, 0))],
-       2: [('s', ('w', 1, 0)), ('s', ('v', 0, 1))],
-       3: [('s', ('v', 0, 0))],
-       4: [('s', ('x', 1, 0)), ('s', ('x', 1, 1))]},
- 'tags': ['h', 'tr', 'h', 'tr', 'mx', 'h'],
- 'ts': 0,
- 'v': {},
- 'z6': 1}
+TENSOR_STEPS = range(1, 6)
+VECTOR_COPY_STEP = 5
+
+GPSIMD_COPIES = [("v", 0, 0), ("x", 1, 0), ("w", K, 1), ("w", Q, 0), ("w", V, 0), ("x", 0, 1), ("z", 1, 0)]
+SCALAR_COPIES = {
+    0: [("x", 1, 1)],
+    1: [("w", K, 0)],
+    2: [("z", 0, 0), ("w", Q, 1)],
+    3: [("w", V, 1)],
+    4: [("x", 0, 0), ("v", 1, 0)],
+    5: [("z", 2, 0)],
+}
+GRAD2_HALVES = {0: [(0, 0), (0, 1)], 4: [(1, 1)], 6: [(1, 0)]}
+EARLY_TILES = {
+    5: [(("dx", 0, 3), "mx"), (("dx", 0, 0), "h")],
+    6: [(("dx", 0, 2), "mx"), (("dw", V, 0), "d"), (("dw", V, 3), "mx")],
+}
+LATE_TILES = {
+    5: [(("dx", 0, 1), "mx")],
+    6: [(("dw", V, 1), "h"), (("dw", V, 2), "mx"), (("dw", Q, 3), "h"), (("dw", Q, 2), "mx"), (("dw", Q, 1), "h")],
+}
+VECTOR_BANKS = {
+    ("dx", 0, 2): (0, 1),
+    ("dx", 1, 1): (0,),
+    ("dw", K, 0): (0, 1),
+    ("dw", K, 2): (1,),
+    ("dw", K, 1): (1,),
+    ("dx", 1, 3): (0, 1),
+    ("dx", 1, 2): (0,),
+}
 
 
 def tile_attentionhead_pa_v_kernel(tc, x, W_qkv, sqk, q1, k1, grad_0, grad_1, grad_2, out_0, out_1):
     nc = tc.nc
     saved = [q1, k1]
     grads = [grad_0, grad_1, grad_2]
+    by_scalar, by_vector = nc.scalar.copy, nc.vector.tensor_copy
 
     with ExitStack() as ctx:
         keep = ctx.enter_context(tc.tile_pool(name="keep", bufs=1))
         work = ctx.enter_context(tc.tile_pool(name="work", bufs=2))
-        ps_h = ctx.enter_context(tc.psum_pool(name="ps_h", bufs=2))
-        ps_t = ctx.enter_context(tc.psum_pool(name="ps_t", bufs=2))
-        ps_mx = ctx.enter_context(tc.psum_pool(name="ps_mx", bufs=2))
-        ps_c = ctx.enter_context(tc.psum_pool(name="ps_c", bufs=1))
+        pools = {tag: ctx.enter_context(tc.psum_pool(name="ps_" + tag, bufs=2)) for tag in ("h", "d", "tr", "mx")}
         ctx.enter_context(tc.manual_schedule())
 
-        zrow = keep.tile([P, D], BF16, name="zrow")
-        nc.vector.memset(zrow[:], 0.0)
+        gain_row = keep.tile([P, D], BF16, name="gain_row")
+        nc.vector.memset(gain_row[:], 0.0)
         ones = keep.tile([P, P], BF16, name="ones")
         nc.gpsimd.memset(ones[:], 1.0)
-        pos = keep.tile([P, J], F32, name="pos")
-        nc.gpsimd.iota(pos[:], [[1, J]], base=0, channel_multiplier=J, allow_small_or_imprecise_dtypes=True)
+        position = keep.tile([P, J], F32, name="position")
+        nc.gpsimd.iota(position[:], [[1, J]], base=0, channel_multiplier=J, allow_small_or_imprecise_dtypes=True)
         ident_b = keep.tile([P, P], BF16, name="ident_b")
         make_identity(nc, ident_b[:])
         ident_f = keep.tile([P, P], F32, name="ident_f")
@@ -75,17 +83,17 @@ def tile_attentionhead_pa_v_kernel(tc, x, W_qkv, sqk, q1, k1, grad_0, grad_1, gr
 
         g_t, u_t, g2_t, x_t, w_t = {}, {}, {}, {}, {}
 
-        def load_unit(n, parts):
-            s, b = UNITS[n]
-            g_t[n] = work.tile([P, J, D], BF16, tag="g", name="g", bufs=2)
-            u_t[n] = work.tile([P, J, D], F32, tag="u", name="u", bufs=3)
-            w = J // parts
-            for h in range(parts):
-                for t, src in ((g_t[n], grads[s]), (u_t[n], saved[s])):
-                    view = src[b].rearrange("(p j) w -> p j w", j=J)
-                    nc.sync.dma_start(out=t[:, h * w : (h + 1) * w, :], in_=view[:, h * w : (h + 1) * w, :])
+        def load_unit(unit, parts):
+            s, b = UNITS[unit]
+            g_t[unit] = work.tile([P, J, D], BF16, tag="g", name="g", bufs=2)
+            u_t[unit] = work.tile([P, J, D], F32, tag="u", name="u", bufs=3)
+            width = J // parts
+            for part in range(parts):
+                js = slice(part * width, (part + 1) * width)
+                for tile, source in ((g_t[unit], grads[s]), (u_t[unit], saved[s])):
+                    nc.sync.dma_start(out=tile[:, js, :], in_=source[b].rearrange("(p j) w -> p j w", j=J)[:, js, :])
 
-        def load_g2(b):
+        def load_grad2(b):
             g2_t[b] = work.tile([P, J, D], BF16, tag="g2", name="g2", bufs=2)
             nc.sync.dma_start(out=g2_t[b][:], in_=grad_2[b].rearrange("(p j) w -> p j w", j=J))
 
@@ -97,24 +105,24 @@ def tile_attentionhead_pa_v_kernel(tc, x, W_qkv, sqk, q1, k1, grad_0, grad_1, gr
             w_t[s] = work.tile([P, J, C], BF16, tag="xw", name="w_in", bufs=4)
             nc.sync.dma_start(out=w_t[s][:], in_=W_qkv[s * D : (s + 1) * D, :].rearrange("(p j) c -> p j c", j=J))
 
-        nc.sync.dma_start(out=zrow[0:1, :], in_=sqk.rearrange("(o n) -> o n", o=1))
+        nc.sync.dma_start(out=gain_row[0:1, :], in_=sqk.rearrange("(o n) -> o n", o=1))
         load_unit(0, 2)
-        load_w(2)
+        load_grad2(0)
         load_unit(1, 1)
-        load_w(0)
-        load_g2(0)
-        load_w(1)
-        load_unit(2, 1)
-        load_x(0)
-        load_g2(1)
         load_x(1)
+        load_w(K)
+        load_unit(2, 1)
+        load_w(V)
+        load_w(Q)
+        load_grad2(1)
         load_unit(3, 1)
+        load_x(0)
 
         diag = keep.tile([P, 4, P], BF16, name="diag")
-        gain_ps = ps_h.tile([P, D], F32, tag="h", name="gain_ps")
-        nc.tensor.matmul(gain_ps[:], lhsT=ones[:], rhs=zrow[:], start=True, stop=True)
+        gain_ps = pools["h"].tile([P, D], F32, tag="h", name="gain_ps")
+        nc.tensor.matmul(gain_ps[:], lhsT=ones[:], rhs=gain_row[:], start=True, stop=True)
 
-        def gain_diag():
+        def make_diag():
             nc.vector.tensor_tensor(
                 out=diag[:],
                 in0=ident_b[:].unsqueeze(1).to_broadcast([P, 4, P]),
@@ -122,437 +130,378 @@ def tile_attentionhead_pa_v_kernel(tc, x, W_qkv, sqk, q1, k1, grad_0, grad_1, gr
                 op=ALU.mult,
             )
 
-        step16 = keep.tile([P, 2, 16], F32, name="step16")
-        for half, first in enumerate((1.0 / (2.0 * math.pi), 1.0)):
-            nc.vector.tensor_scalar(out=step16[:, half, 0:1], in0=pos[:, 0:1], scalar1=0.0, scalar2=first, op0=ALU.mult, op1=ALU.add)
+        fine_coarse = keep.tile([P, 2, 16], F32, name="fine_coarse")
+        for row, first in enumerate((1.0 / (2.0 * math.pi), 1.0)):
+            nc.vector.tensor_scalar(out=fine_coarse[:, row, 0:1], in0=position[:, 0:1], scalar1=0.0, scalar2=first, op0=ALU.mult, op1=ALU.add)
         for k in range(4):
             n = 1 << k
-            for half, unit in enumerate((1.0, 16.0)):
-                nc.vector.tensor_scalar_mul(step16[:, half, n : 2 * n], step16[:, half, 0:n], ROPE_BASE ** (-unit * n / H))
+            for row, stride in enumerate((1.0, 16.0)):
+                nc.vector.tensor_scalar_mul(fine_coarse[:, row, n : 2 * n], fine_coarse[:, row, 0:n], ROPE_BASE ** (-stride * n / H))
         freq = keep.tile([P, H], F32, name="freq")
         nc.vector.tensor_tensor(
-            out=freq[:].rearrange("p (a b) -> p a b", a=16),
-            in0=step16[:, 1, :].unsqueeze(2).to_broadcast([P, 16, 16]),
-            in1=step16[:, 0, :].unsqueeze(1).to_broadcast([P, 16, 16]),
+            out=freq[:].rearrange("p (a c) -> p a c", a=16),
+            in0=fine_coarse[:, 1, :].unsqueeze(2).to_broadcast([P, 16, 16]),
+            in1=fine_coarse[:, 0, :].unsqueeze(1).to_broadcast([P, 16, 16]),
             op=ALU.mult,
         )
-        tau = work.tile([P, J, H], F32, tag="A", name="tau")
+        turns = work.tile([P, J, H], F32, tag="A", name="turns")
         whole = work.tile([P, J, H], I32, tag="B", name="whole")
-        frac = work.tile([P, J, H], F32, tag="A", name="frac")
-        mag = work.tile([P, J, H], F32, tag="B", name="mag")
+        rest = work.tile([P, J, H], F32, tag="A", name="rest")
+        rest_abs = work.tile([P, J, H], F32, tag="B", name="rest_abs")
         halves = [slice(0, 2), slice(2, 4)]
         for j in range(J):
-            nc.vector.tensor_scalar_mul(tau[:, j, :], freq[:], pos[:, j : j + 1])
+            nc.vector.tensor_scalar_mul(turns[:, j, :], freq[:], position[:, j : j + 1])
         for js in halves:
-            nc.vector.tensor_copy(out=whole[:, js, :], in_=tau[:, js, :])
-        def reduce_angle(h):
-            js = halves[h]
-            nc.vector.tensor_tensor(out=frac[:, js, :], in0=tau[:, js, :], in1=whole[:, js, :], op=ALU.subtract)
+            nc.vector.tensor_copy(out=whole[:, js, :], in_=turns[:, js, :])
 
-        def magnitude(h):
-            js = halves[h]
-            nc.vector.scalar_tensor_tensor(out=mag[:, js, :], in0=frac[:, js, :], scalar=-1.0, in1=frac[:, js, :], op0=ALU.mult, op1=ALU.max)
+        def take_rest(half):
+            js = halves[half]
+            nc.vector.tensor_tensor(out=rest[:, js, :], in0=turns[:, js, :], in1=whole[:, js, :], op=ALU.subtract)
 
-        reduce_angle(0)
-        gain_diag()
-        magnitude(0)
-        reduce_angle(1)
+        def take_abs(half):
+            js = halves[half]
+            nc.vector.scalar_tensor_tensor(out=rest_abs[:, js, :], in0=rest[:, js, :], scalar=-1.0, in1=rest[:, js, :], op0=ALU.mult, op1=ALU.max)
+
+        take_rest(0)
+        make_diag()
+        take_abs(0)
+        take_rest(1)
         sin_t = keep.tile([P, J, H], F32, name="sin_t")
         cos_t = keep.tile([P, J, H], F32, name="cos_t")
         warm = keep.tile([P, 1], F32, name="warm")
-        nc.scalar.activation(out=warm[:], in_=pos[:, 0:1], func=ACT.Sin, scale=0.0)
+        nc.scalar.activation(out=warm[:], in_=position[:, 0:1], func=ACT.Sin, scale=0.0)
 
-        cos_ps = []
+        def tables(half):
+            js = halves[half]
+            nc.scalar.activation(out=cos_t[:, js, :], in_=rest_abs[:, js, :], func=ACT.Sin, scale=-2.0 * math.pi, bias=math.pi / 2.0)
+            nc.scalar.activation(out=sin_t[:, js, :], in_=rest[:, js, :], func=ACT.Sin, scale=2.0 * math.pi)
 
-        def tables(h):
-            js = halves[h]
-            nc.scalar.activation(out=cos_t[:, js, :], in_=mag[:, js, :], func=ACT.Sin, scale=-2.0 * math.pi, bias=math.pi / 2.0)
-            nc.scalar.activation(out=sin_t[:, js, :], in_=frac[:, js, :], func=ACT.Sin, scale=2.0 * math.pi)
-            cos_ps.append(ps_c.tile([P, 2, H], F32, tag="cos%d" % h, name="cos_ps"))
-            nc.tensor.matmul(
-                cos_ps[h][:].rearrange("p j w -> p (j w)"), lhsT=ident_f[:],
-                rhs=cos_t[:, js, :].rearrange("p j w -> p (j w)"), start=True, stop=True,
-            )
+        def mx_operand(name, width):
+            codes = keep.tile([P, width], U32, name=name + "_c", align_bytes=64)
+            scales = keep.tile([P, width], U8, name=name + "_s", align_bytes=64)
+            return codes, scales
 
-        def codes(tag, width):
-            c = keep.tile([P, width], U32, name=tag + "_c", align_bytes=64)
-            s = keep.tile([P, width], U8, name=tag + "_s", align_bytes=64)
-            return c, s
+        x_q = [mx_operand("x%d" % b, C) for b in range(B)]
+        w_q = [mx_operand("w%d" % s, C) for s in range(3)]
+        tok_q = [[mx_operand("t%d%d" % (s, b), D) for b in range(B)] for s in range(3)]
+        fea_q = [[mx_operand("f%d%d" % (s, b), D) for b in range(B)] for s in range(3)]
 
-        x_q = [codes("x%d" % b, C) for b in range(B)]
-        w_q = [codes("w%d" % s, C) for s in range(3)]
-        tok_q = [[codes("t%d%d" % (s, b), D) for b in range(B)] for s in range(3)]
-        fea_q = [[codes("f%d%d" % (s, b), D) for b in range(B)] for s in range(3)]
+        def quantize(operand, lo, width, values, fmt):
+            nc.vector.quantize_mx(out=operand[0][:, lo : lo + width].bitcast(fmt), scales=operand[1][:, lo : lo + width], in_=values)
 
-        def quantize(dst, lo, width, stage, fmt):
-            nc.vector.quantize_mx(
-                out=dst[0][:, lo : lo + width].bitcast(fmt),
-                scales=dst[1][:, lo : lo + width],
-                in_=stage,
-            )
-
-        def interleave(copy, dst, src):
-            copy(out=dst.rearrange("p (c i t) -> p c t i", i=4, t=J), in_=src.rearrange("p t (c i) -> p c t i", i=4))
+        def interleave(copy, out, in_):
+            copy(out=out.rearrange("p (c i t) -> p c t i", i=4, t=J), in_=in_.rearrange("p t (c i) -> p c t i", i=4))
 
         staged = {}
 
-        def by_pe(out, in_):
-            for h in range(2):
-                tr = ps_t.tile([P, 256, J], BF16, tag="tr", name="itr")
-                for q in range(2):
-                    lo = h * 256 + q * P
-                    nc.tensor.matmul(
-                        tr[:, q * P : (q + 1) * P, :].rearrange("p c t -> p (c t)"), lhsT=ident_b[:],
-                        rhs=in_[:, :, lo : lo + P].rearrange("p t c -> p c t"), start=True, stop=True,
-                    )
-                nc.scalar.copy(out=out[:, h * 1024 : (h + 1) * 1024], in_=tr[:].rearrange("p c t -> p (c t)"))
-
-        def source(key):
-            kind, a, n = key
+        def slots_of(piece):
+            kind, index, half = piece
+            cols = slice(half * D, (half + 1) * D)
             if kind == "x":
-                return x_t[a][:, :, n * D : (n + 1) * D]
+                return x_t[index][:, :, cols]
             if kind == "w":
-                return w_t[a][:, :, n * D : (n + 1) * D]
-            return g2_t[n][:] if kind == "v" else z_t[a][:]
+                return w_t[index][:, :, cols]
+            return g2_t[index][:] if kind == "v" else z_t[index][:]
 
-        def stage_piece(copy, key):
-            st = work.tile([P, J * D], BF16, tag="stage", name="stage", bufs=4, align_bytes=64)
-            src = source(key)
-            if copy is None:
-                by_pe(st[:], src)
-            else:
-                interleave(copy, st[:], src)
-            staged[key] = st
+        def scalar_copy(piece):
+            staged[piece] = work.tile([P, J * D], BF16, tag="stage", name="stage", bufs=4, align_bytes=64)
+            interleave(by_scalar, staged[piece][:], slots_of(piece))
 
-        def quant_piece(key):
-            kind, a, n = key
-            st = staged[key]
+        def quantize_piece(piece):
+            kind, index, half = piece
+            values = staged[piece][:]
             if kind == "x":
-                quantize(x_q[a], n * D, D, st[:], E4M3)
+                quantize(x_q[index], half * D, D, values, E4M3)
             elif kind == "w":
-                quantize(w_q[a], n * D, D, st[:], E4M3)
-            elif kind == "v":
-                quantize(tok_q[2][n], 0, D, st[:], E5M2)
+                quantize(w_q[index], half * D, D, values, E4M3)
             else:
-                s, b = UNITS[a]
-                quantize(tok_q[s][b], 0, D, st[:], E5M2)
+                s, b = (V, index) if kind == "v" else UNITS[index]
+                quantize(tok_q[s][b], 0, D, values, E5M2)
 
-        z_t, gT, h_t, ss, rr, rt, dots, nal, d_t, a_t, b_t = {}, {}, {}, {}, {}, {}, {}, {}, {}, {}, {}
+        gpsimd_todo = list(GPSIMD_COPIES)
+        gpsimd_done = []
 
-        gtr = {}
+        def window():
+            if gpsimd_done:
+                quantize_piece(gpsimd_done.pop())
+            if gpsimd_todo:
+                piece = gpsimd_todo.pop(0)
+                staged[piece] = work.tile([P, J * D], BF16, tag="gs", name="gs", bufs=1, align_bytes=64)
+                nc.gpsimd.tensor_scalar(
+                    out=staged[piece][:].rearrange("p (c t) -> p c t", t=J),
+                    in0=slots_of(piece).rearrange("p t c -> p c t"),
+                    scalar1=1.0, scalar2=0.0, op0=ALU.mult, op1=ALU.add,
+                )
+                gpsimd_done.append(piece)
+
+        z_t, g_tr, g_sb, h_t, ss, rr, rt, dots, alphas, d_rows, a_t, b_t = {}, {}, {}, {}, {}, {}, {}, {}, {}, {}, {}, {}
+
+        def slot(i, jj):
+            return 2 * (i % 2) + jj
 
         def grad_transpose(i, parts=1):
-            gtr[i] = []
-            for q in range(parts):
-                tr = ps_t.tile([P, 2 // parts, 4, P], BF16, tag="tr", name="gtr")
+            g_tr[i] = []
+            for part in range(parts):
+                tr = pools["tr"].tile([P, 2 // parts, 4, P], BF16, tag="tr", name="gtr")
                 for jj in range(2 // parts):
                     for f in range(4):
-                        j = 2 * (i % 2) + 2 * q // parts + jj
-                        nc.tensor.transpose(tr[:, jj, f, :], g_t[i // 2][:, j, f * P : (f + 1) * P], ident_b[:])
-                gtr[i].append(tr)
+                        block = g_t[i // 2][:, slot(i, 2 * part // parts + jj), f * P : (f + 1) * P]
+                        nc.tensor.transpose(tr[:, jj, f, :], block, ident_b[:])
+                g_tr[i].append(tr)
 
         def grad_copy(i, copy):
-            gT[i] = work.tile([P, 2, 4, P], BF16, tag="gT", name="gT", bufs=2)
-            n = 2 // len(gtr[i])
-            for q, tr in enumerate(gtr[i]):
-                copy(out=gT[i][:, q * n : (q + 1) * n, :, :], in_=tr[:])
+            g_sb[i] = work.tile([P, 2, 4, P], BF16, tag="gT", name="gT", bufs=2)
+            n = 2 // len(g_tr[i])
+            for part, tr in enumerate(g_tr[i]):
+                copy(out=g_sb[i][:, part * n : (part + 1) * n, :, :], in_=tr[:])
 
-        def gain(i):
+        def gain_matmuls(i, jj, out, stop):
+            for f in range(4):
+                nc.tensor.matmul(
+                    out[:, f * P : (f + 1) * P], lhsT=g_sb[i][:, jj, f, :], rhs=diag[:, f, :], start=(f == 0), stop=(stop and f == 3)
+                )
+
+        def apply_gain(i):
             for jj in range(2):
-                h = ps_h.tile([P, D], F32, tag="h", name="h")
-                for f in range(4):
-                    nc.tensor.matmul(h[:, f * P : (f + 1) * P], lhsT=gT[i][:, jj, f, :], rhs=diag[:, f, :], start=True, stop=True)
-                h_t[i, jj] = h
+                h_t[i, jj] = pools["h"].tile([P, D], F32, tag="h", name="h")
+                gain_matmuls(i, jj, h_t[i, jj], True)
 
         def squares(i):
             ss[i] = work.tile([P, 2], F32, tag="ss", name="ss", bufs=3)
             for jj in range(2):
-                sq = work.tile([P, D], BF16, tag="sq", name="sq")
-                nc.scalar.activation(out=sq[:], in_=u_t[i // 2][:, 2 * (i % 2) + jj, :], func=ACT.Square, accum_out=ss[i][:, jj : jj + 1])
+                unread = work.tile([P, D], BF16, tag="sq", name="sq")
+                nc.scalar.activation(out=unread[:], in_=u_t[i // 2][:, slot(i, jj), :], func=ACT.Square, accum_out=ss[i][:, jj : jj + 1])
 
-        def recip(i):
+        def norm_square_reciprocal(i):
             rr[i] = work.tile([P, 2], F32, tag="rr", name="rr", bufs=3)
             nc.vector.reciprocal(rr[i][:], ss[i][:])
 
-        def root(i):
+        def norm_reciprocal(i):
             rt[i] = work.tile([P, 2], F32, tag="rt", name="rt", bufs=3)
             nc.scalar.activation(out=rt[i][:], in_=rr[i][:], func=ACT.Sqrt)
 
         def dot(i, jj):
             if jj == 0:
                 dots[i] = work.tile([P, 2], F32, tag="dots", name="dots", bufs=3)
-            prod = work.tile([P, D], F32, tag="prod", name="prod")
+            unread = work.tile([P, D], F32, tag="prod", name="prod")
             nc.vector.scalar_tensor_tensor(
-                out=prod[:], in0=h_t[i, jj][:], scalar=1.0, in1=u_t[i // 2][:, 2 * (i % 2) + jj, :],
+                out=unread[:], in0=h_t[i, jj][:], scalar=1.0, in1=u_t[i // 2][:, slot(i, jj), :],
                 op0=ALU.mult, op1=ALU.mult, accum_out=dots[i][:, jj : jj + 1],
             )
 
         def alpha(i):
-            nal[i] = work.tile([P, 2], F32, tag="nal", name="nal", bufs=3)
+            alphas[i] = work.tile([P, 2], F32, tag="nal", name="nal", bufs=3)
             for jj in range(2):
                 col = slice(jj, jj + 1)
-                nc.vector.tensor_scalar(out=nal[i][:, col], in0=dots[i][:, col], scalar1=rr[i][:, col], scalar2=-1.0, op0=ALU.mult, op1=ALU.mult)
+                nc.vector.tensor_scalar(out=alphas[i][:, col], in0=dots[i][:, col], scalar1=rr[i][:, col], scalar2=-1.0, op0=ALU.mult, op1=ALU.mult)
 
         def project(i, jj):
-            if jj == 0:
-                d_t[i] = work.tile([P, 2, D], F32, tag="d", name="d")
-            nc.vector.scalar_tensor_tensor(
-                out=d_t[i][:, jj, :], in0=u_t[i // 2][:, 2 * (i % 2) + jj, :], scalar=nal[i][:, jj : jj + 1], in1=h_t[i, jj][:],
-                op0=ALU.mult, op1=ALU.add,
-            )
+            u_rows, col = u_t[i // 2][:, slot(i, jj), :], slice(jj, jj + 1)
+            if i in TENSOR_STEPS:
+                alpha_diag = work.tile([P, P], F32, tag="alpha_diag", name="alpha_diag")
+                nc.scalar.activation(out=alpha_diag[:], in_=ident_f[:], func=ACT.Copy, scale=alphas[i][:, col])
+                d_ps = pools["d"].tile([P, D], F32, tag="d", name="d_ps")
+                gain_matmuls(i, jj, d_ps, False)
+                nc.tensor.matmul(d_ps[:], lhsT=alpha_diag[:], rhs=u_rows, start=False, stop=True)
+                d_rows[i, jj] = d_ps[:]
+            else:
+                d_sb = work.tile([P, D], F32, tag="d", name="d_sb", bufs=4)
+                nc.vector.scalar_tensor_tensor(out=d_sb[:], in0=u_rows, scalar=alphas[i][:, col], in1=h_t[i, jj][:], op0=ALU.mult, op1=ALU.add)
+                d_rows[i, jj] = d_sb[:]
 
-        def times(i, jj, table, store, tag, lo=0, hi=H):
-            if jj == 0 and lo == 0:
+        def times(i, table, store, tag, lo=0, hi=H):
+            if lo == 0:
                 store[i] = work.tile([P, 2, D], F32, tag=tag, name=tag)
-            nc.vector.scalar_tensor_tensor(
-                out=store[i][:, jj, :].rearrange("p (h w) -> p h w", h=2)[:, :, lo:hi],
-                in0=d_t[i][:, jj, :].rearrange("p (h w) -> p h w", h=2)[:, :, lo:hi],
-                scalar=rt[i][:, jj : jj + 1],
-                in1=table[:, jj, lo:hi].unsqueeze(1).to_broadcast([P, 2, hi - lo]),
-                op0=ALU.mult, op1=ALU.mult,
-            )
+            for jj in range(2):
+                nc.vector.scalar_tensor_tensor(
+                    out=store[i][:, jj, :].rearrange("p (h w) -> p h w", h=2)[:, :, lo:hi],
+                    in0=d_rows[i, jj].rearrange("p (h w) -> p h w", h=2)[:, :, lo:hi],
+                    scalar=rt[i][:, jj : jj + 1],
+                    in1=table[:, jj, lo:hi].unsqueeze(1).to_broadcast([P, 2, hi - lo]),
+                    op0=ALU.mult, op1=ALU.mult,
+                )
+
+        def times_cos(i, lo=0, hi=H):
+            times(i, cos_t[:, halves[i % 2], :], a_t, "A", lo, hi)
+
+        def times_sin(i, lo=0, hi=H):
+            times(i, sin_t[:, halves[i % 2], :], b_t, "B", lo, hi)
 
         def rotate(i, lo=0, hi=H):
             if i % 2 == 0:
                 z_t[i // 2] = work.tile([P, J, D], BF16, tag="z", name="z", align_bytes=64)
-            js = slice(2 * (i % 2), 2 * (i % 2) + 2)
+            js = halves[i % 2]
             z, a, b = z_t[i // 2], a_t[i], b_t[i]
             one, two = slice(lo, hi), slice(H + lo, H + hi)
             nc.vector.tensor_tensor(out=z[:, js, one], in0=a[:, :, one], in1=b[:, :, two], op=ALU.add)
             nc.vector.tensor_tensor(out=z[:, js, two], in0=a[:, :, two], in1=b[:, :, one], op=ALU.subtract)
 
-        fst = {}
+        z_tr, z_fea = {}, {}
 
-        def fea_transpose(key, copy=nc.scalar.copy):
-            if isinstance(key, int):
-                src, half = z_t[key // 2], key % 2
-            else:
-                src, half = g2_t[key[1]], key[2]
-            words = src[:].rearrange("p j w -> p (j w)").bitcast(F32)
-            tr = ps_t.tile([P, 2, 2, P], F32, tag="tr", name="ztr")
+        def step_key(i):
+            return UNITS[i // 2] + (i % 2,)
+
+        def fea_transpose(key):
+            s, b, half = key
+            rows = g2_t[b] if s == V else z_t[UNITS.index((s, b))]
+            words = rows[:].rearrange("p j w -> p (j w)").bitcast(F32)
+            tr = pools["tr"].tile([P, 2, 2, P], F32, tag="tr", name="ztr")
             for jj in range(2):
                 lo = (2 * half + jj) * H
                 for e in range(2):
                     nc.tensor.transpose(tr[:, jj, e, :], words[:, lo + e : lo + H : 2], ident_f[:])
-            fst[key] = work.tile([P, J * H], BF16, tag="fst", name="fst", bufs=3, align_bytes=64)
+            z_tr[key] = tr
+
+        def fea_copy(key, copy):
+            z_fea[key] = work.tile([P, J * H], BF16, tag="fst", name="fst", bufs=3, align_bytes=64)
             copy(
-                out=fst[key][:].bitcast(F32).rearrange("p (j t e) -> p j t e", j=2, e=2),
-                in_=tr[:].rearrange("p j e t -> p j t e"),
+                out=z_fea[key][:].bitcast(F32).rearrange("p (j t e) -> p j t e", j=2, e=2),
+                in_=z_tr[key][:].rearrange("p j e t -> p j t e"),
             )
 
-        def fea_quant(key):
-            if isinstance(key, int):
-                s, b = UNITS[key // 2]
-                half = key % 2
-            else:
-                s, b, half = 2, key[1], key[2]
-            quantize(fea_q[s][b], half * H, H, fst[key][:], E5M2)
+        def fea_quantize(key):
+            s, b, half = key
+            quantize(fea_q[s][b], half * H, H, z_fea[key][:], E5M2)
 
-        def passes(accs, lhs, rhs, lo, which, count):
+        def operands(item):
+            kind, index, n = item
+            if kind == "dw":
+                row = index * D + n * P
+                return tok_q[index], x_q, n * P, out_1[row : row + P, :]
+            order = (V, Q, K)
+            rows = out_0[index].rearrange("(p j) c -> p j c", j=J)[:, n, :]
+            return [fea_q[s][index] for s in order], [w_q[s] for s in order], n * P, rows
+
+        def passes(item, accs):
+            lhs, rhs, lo, rows = operands(item)
             for n in range(2):
-                for k in which:
+                cols = slice(n * D, (n + 1) * D)
+                for k in range(len(lhs)):
                     nc.tensor.matmul_mx(
                         out=accs[n][:],
                         lhsT=lhs[k][0][:, lo : lo + P].bitcast(E5M2),
                         lhsT_scale=lhs[k][1][:, lo : lo + P],
-                        rhs=rhs[k][0][:, n * D : (n + 1) * D].bitcast(E4M3),
-                        rhs_scale=rhs[k][1][:, n * D : (n + 1) * D],
+                        rhs=rhs[k][0][:, cols].bitcast(E4M3),
+                        rhs_scale=rhs[k][1][:, cols],
                         start=(k == 0),
-                        stop=(k == count - 1),
+                        stop=(k == len(lhs) - 1),
                     )
 
-        pools = {"h": ps_h, "mx": ps_mx, "tr": ps_t}
-
-        def accs_of(tag):
-            pool = pools[tag]
-            a0 = pool.tile([P, D], F32, tag=tag, name="acc0")
-            a1 = pool.tile([P, D], F32, tag=tag, name="acc1")
-            return a0, a1
-
-        def empty(accs, dest, engines):
+        def output_tile(item, tag, stores=1):
+            accs = [pools[tag].tile([P, D], F32, tag=tag, name="acc") for n in range(2)]
+            passes(item, accs)
+            rows = operands(item)[3]
             o = work.tile([P, C], F32, tag="o", name="o", bufs=5)
             for n in range(2):
-                engines[n](out=o[:, n * D : (n + 1) * D], in_=accs[n][:])
-                if halves_out:
-                    nc.sync.dma_start(out=dest[:, n * D : (n + 1) * D], in_=o[:, n * D : (n + 1) * D])
-            if not halves_out:
-                nc.sync.dma_start(out=dest, in_=o[:])
+                cols = slice(n * D, (n + 1) * D)
+                copy = by_vector if n in VECTOR_BANKS.get(item, ()) else by_scalar
+                copy(out=o[:, cols], in_=accs[n][:])
+                if stores == 2:
+                    nc.sync.dma_start(out=rows[:, cols], in_=o[:, cols])
+            if stores == 1:
+                nc.sync.dma_start(out=rows, in_=o[:])
 
-        halves_out = []
-
-        def operands(item):
-            kind, a, n = item
-            if kind == "w":
-                r = a * D + n * P
-                return tok_q[a], x_q, n * P, out_1[r : r + P, :]
-            view = out_0[a].rearrange("(p j) c -> p j c", j=J)
-            return [fea_q[s][a] for s in (2, 0, 1)], [w_q[s] for s in (2, 0, 1)], n * P, view[:, n, :]
-
-        def mx_begin(item, tag):
-            lhs, rhs, lo, dest = operands(item)
-            accs = accs_of(tag)
-            passes(accs, lhs, rhs, lo, range(len(lhs) - 1), len(lhs))
-            return accs
-
-        def mx_finish(item, accs, engines):
-            lhs, rhs, lo, dest = operands(item)
-            passes(accs, lhs, rhs, lo, [len(lhs) - 1], len(lhs))
-            empty(accs, dest, engines)
-
-        def do_mx(item, engines, tag="mx"):
-            lhs, rhs, lo, dest = operands(item)
-            accs = accs_of(tag)
-            passes(accs, lhs, rhs, lo, range(len(lhs)), len(lhs))
-            empty(accs, dest, engines)
-
-        sc, ve = nc.scalar.copy, nc.vector.tensor_copy
-
-        g_last = []
-
-        def window():
-            if g_last:
-                quant_piece(g_last.pop())
-            if g_fill:
-                key = g_fill.pop(0)
-                st = work.tile([P, J * D], BF16, tag="gs", name="gs", bufs=1, align_bytes=64)
-                nc.gpsimd.tensor_scalar(
-                    out=st[:].rearrange("p (c t) -> p c t", t=J),
-                    in0=source(key).rearrange("p t c -> p c t"),
-                    scalar1=1.0, scalar2=0.0, op0=ALU.mult, op1=ALU.add,
-                )
-                staged[key] = st
-                g_last.append(key)
-
-        g_fill = list(PLAN["g"])
-        s_fill, v_fill, mx_plan = PLAN["s"], PLAN["v"], PLAN["mx"]
-        v_feats = {1: [("v", 0, 0), ("v", 0, 1)], 4: [("v", 1, 0), ("v", 1, 1)]}
-
-        last = STEPS - 1
         grad_transpose(0, 2)
-        grad_copy(0, sc)
-        gain(0)
+        grad_copy(0, by_scalar)
+        apply_gain(0)
         grad_transpose(1)
         squares(0)
         tables(0)
         dot(0, 0)
         dot(0, 1)
-        recip(0)
-        magnitude(1)
+        norm_square_reciprocal(0)
+        take_abs(1)
         alpha(0)
-        grad_copy(1, ve)
+        grad_copy(1, by_vector)
         project(0, 0)
         project(0, 1)
-        gain(1)
+        apply_gain(1)
         squares(1)
         tables(1)
-        root(0)
-        recip(1)
-        root(1)
+        norm_reciprocal(0)
+        norm_square_reciprocal(1)
+        norm_reciprocal(1)
 
-        pending = []
         window()
-        for i in range(last):
+        to_quantize = []
+        for i in range(LAST):
             nxt, pre = i + 1, i + 2
-            if i > 0:
-                fea_transpose(i - 1)
+            grad2_keys = [(V, b, half) for b, half in GRAD2_HALVES.get(i, [])]
             if pre < STEPS:
                 grad_transpose(pre)
-                if not PLAN["gt"]:
-                    grad_copy(pre, sc)
-            for key in v_feats.get(i, []):
-                fea_transpose(key)
-            if i > 0:
-                root(nxt)
             dot(nxt, 0)
             dot(nxt, 1)
-            if pre < STEPS and PLAN["gt"]:
-                grad_copy(pre, ve)
             if pre < STEPS:
-                squares(pre)
+                grad_copy(pre, by_vector if pre == VECTOR_COPY_STEP else by_scalar)
+            for item, tag in EARLY_TILES.get(i, []):
+                output_tile(item, tag)
+            if i > 0:
+                norm_reciprocal(nxt)
+            for key in grad2_keys:
+                fea_transpose(key)
+                fea_copy(key, by_scalar)
             alpha(nxt)
+            if i > 0:
+                fea_transpose(step_key(i - 1))
+            if pre < STEPS:
+                apply_gain(pre)
             project(nxt, 0)
             project(nxt, 1)
-            for e, key in PLAN["e"].get(i, []):
-                stage_piece(sc if e == "s" else None, key)
-            for item in mx_plan.get(i, []):
-                do_mx(item[:3], (sc, ve if item[3] else sc))
-            for jj in range(2):
-                times(i, jj, cos_ps[i % 2], a_t, "A")
-            for jj in range(2):
-                times(i, jj, sin_t[:, 2 * (i % 2) : 2 * (i % 2) + 2, :], b_t, "B")
             if pre < STEPS:
-                gain(pre)
-            for key in v_fill.get(i, []):
-                stage_piece(ve, key)
-            if i > 0:
-                fea_quant(i - 1)
-            for key in v_feats.get(i, []):
-                fea_quant(key)
-            if pre < STEPS:
-                recip(pre)
-            for key in pending + [k for e, k in PLAN["e"].get(i, [])] + v_fill.get(i, []):
-                quant_piece(key)
+                squares(pre)
+            times_cos(i)
+            times_sin(i)
+            for piece in to_quantize:
+                quantize_piece(piece)
+            for key in grad2_keys:
+                fea_quantize(key)
             rotate(i)
+            if i > 0:
+                fea_copy(step_key(i - 1), by_vector if i - 1 == VECTOR_COPY_STEP else by_scalar)
+                fea_quantize(step_key(i - 1))
             window()
-            pending = [k for e, k in s_fill.get(i, [])]
-            for e, key in s_fill.get(i, []):
-                stage_piece(sc if e == "s" else None, key)
-            for n, item in enumerate(mx_plan.get(i + 0.5, [])):
-                do_mx(item[:3], (sc, ve if item[3] else sc), "h" if i == last - 1 and n % 2 == 0 else "mx")
+            for item, tag in LATE_TILES.get(i, []):
+                output_tile(item, tag)
+            to_quantize = SCALAR_COPIES.get(i, [])
+            for piece in to_quantize:
+                scalar_copy(piece)
+            if pre < STEPS:
+                norm_square_reciprocal(pre)
 
-        fea_transpose(last - 1, sc if PLAN["z6"] else ve)
-        while g_last:
-            quant_piece(g_last.pop())
-        for e, key in PLAN["e"].get(last, []):
-            stage_piece(sc if e == "s" else None, key)
-        for key in v_fill.get(last, []):
-            stage_piece(ve, key)
-        for key in pending + [k for e, k in PLAN["e"].get(last, [])] + v_fill.get(last, []):
-            quant_piece(key)
-        st = work.tile([P, J * D], BF16, tag="stage", name="stage", bufs=4, align_bytes=64)
+        stage = work.tile([P, J * D], BF16, tag="stage", name="stage", bufs=4, align_bytes=64)
 
-        def tail_stage(copy, m):
-            interleave(copy, st[:, m * D : (m + 1) * D], z_t[3][:, :, m * P : (m + 1) * P])
+        def block_copy(m):
+            interleave(by_vector, stage[:, m * D : (m + 1) * D], z_t[3][:, :, m * P : (m + 1) * P])
 
-        def tail_quant(m):
-            quantize(tok_q[1][1], m * P, P, st[:, m * D : (m + 1) * D], E5M2)
+        def block_quantize(m):
+            quantize(tok_q[K][1], m * P, P, stage[:, m * D : (m + 1) * D], E5M2)
 
-        def half_times(lo, hi):
-            for jj in range(2):
-                times(last, jj, cos_ps[last % 2], a_t, "A", lo, hi)
-            for jj in range(2):
-                times(last, jj, sin_t[:, 2 * (last % 2) : 2 * (last % 2) + 2, :], b_t, "B", lo, hi)
-
-        half_times(0, P)
-        fea_quant(last - 1)
-        for n, item in enumerate(mx_plan.get(last, [])):
-            do_mx(item[:3], (sc, ve if item[3] else sc), ("h", "mx")[n % 2])
-        half_times(P, H)
-        rotate(last, 0, P)
-        rotate(last, P, H)
-        for n, item in enumerate(mx_plan.get(last + 0.5, [])):
-            do_mx(item[:3], (sc, ve if item[3] else sc), ("h", "mx")[n % 2])
-        open_groups = {}
-        for item, tag in PLAN["open1"]:
-            open_groups[item] = mx_begin(item, tag)
-        tail_stage(ve, 0)
-        tail_stage(ve, 2)
-        fea_transpose(last, sc)
-        for item in mx_plan.get(last + 1, []):
-            do_mx(item[:3], (sc, ve if item[3] else sc), "h")
-        for item, tag in PLAN["open2"]:
-            open_groups[item] = mx_begin(item, tag)
-        tail_stage(ve, 1)
-        tail_quant(0)
-        tail_quant(2)
-        tail_stage(sc if PLAN["ts"] else ve, 3)
-        tail_quant(1)
-        fea_quant(last)
-        tail_quant(3)
-        for n, item in enumerate(PLAN["finish"]):
-            if n == 4:
-                halves_out.append(1)
-            if item in open_groups:
-                mx_finish(item, open_groups[item], (sc, ve))
-            else:
-                do_mx(item, (sc, ve), PLAN["tags"][n])
+        fea_transpose(step_key(LAST - 1))
+        fea_copy(step_key(LAST - 1), by_scalar)
+        times_cos(LAST, 0, P)
+        times_sin(LAST, 0, P)
+        times_sin(LAST, P, H)
+        rotate(LAST, 0, P)
+        fea_quantize(step_key(LAST - 1))
+        block_copy(0)
+        block_copy(2)
+        times_cos(LAST, P, H)
+        block_quantize(0)
+        rotate(LAST, P, H)
+        output_tile(("dw", Q, 0), "d")
+        output_tile(("dx", 1, 1), "h")
+        output_tile(("dx", 1, 0), "d")
+        block_quantize(2)
+        output_tile(("dw", K, 0), "mx")
+        block_copy(3)
+        block_quantize(3)
+        fea_transpose(step_key(LAST))
+        block_copy(1)
+        fea_copy(step_key(LAST), by_scalar)
+        output_tile(("dw", K, 2), "h")
+        output_tile(("dw", K, 3), "d")
+        fea_quantize(step_key(LAST))
+        block_quantize(1)
+        output_tile(("dw", K, 1), "tr")
+        output_tile(("dx", 1, 3), "d")
+        output_tile(("dx", 1, 2), "d", stores=2)

import math
from contextlib import ExitStack

import concourse.mybir as mybir
from concourse.masks import make_identity

F32 = mybir.dt.float32
BF16 = mybir.dt.bfloat16
I32 = mybir.dt.int32
U32 = mybir.dt.uint32
U8 = mybir.dt.uint8
E4M3 = mybir.dt.float8_e4m3fn_x4
E5M2 = mybir.dt.float8_e5m2_x4
ALU = mybir.AluOpType
ACT = mybir.ActivationFunctionType

P = 128
J = 4
B, T, C, D = 2, 512, 1024, 512
H = D // 2
ROPE_BASE = 10000.0
Q, K, V = 0, 1, 2
FLOPS = 2 * 2 * (B * T) * (3 * D) * C

UNITS = [(Q, 0), (K, 0), (Q, 1), (K, 1)]
STEPS = 2 * len(UNITS)
LAST = STEPS - 1

TENSOR_STEPS = range(1, 6)
VECTOR_COPY_STEP = 5

GPSIMD_COPIES = [("v", 0, 0), ("x", 1, 0), ("w", K, 1), ("w", Q, 0), ("w", V, 0), ("x", 0, 1), ("z", 1, 0)]
SCALAR_COPIES = {
    0: [("x", 1, 1)],
    1: [("w", K, 0)],
    2: [("z", 0, 0), ("w", Q, 1)],
    3: [("w", V, 1)],
    4: [("x", 0, 0), ("v", 1, 0)],
    5: [("z", 2, 0)],
}
GRAD2_HALVES = {0: [(0, 0), (0, 1)], 4: [(1, 1)], 6: [(1, 0)]}
EARLY_TILES = {
    5: [(("dx", 0, 3), "mx"), (("dx", 0, 0), "h")],
    6: [(("dx", 0, 2), "mx"), (("dw", V, 0), "d"), (("dw", V, 3), "mx")],
}
LATE_TILES = {
    5: [(("dx", 0, 1), "mx")],
    6: [(("dw", V, 1), "h"), (("dw", V, 2), "mx"), (("dw", Q, 3), "h"), (("dw", Q, 2), "mx"), (("dw", Q, 1), "h")],
}
VECTOR_BANKS = {
    ("dx", 0, 2): (0, 1),
    ("dx", 1, 1): (0,),
    ("dw", K, 0): (0, 1),
    ("dw", K, 2): (1,),
    ("dw", K, 1): (1,),
    ("dx", 1, 3): (0, 1),
    ("dx", 1, 2): (0,),
}


def tile_attentionhead_pa_v_kernel(tc, x, W_qkv, sqk, q1, k1, grad_0, grad_1, grad_2, out_0, out_1):
    nc = tc.nc
    saved = [q1, k1]
    grads = [grad_0, grad_1, grad_2]
    by_scalar, by_vector = nc.scalar.copy, nc.vector.tensor_copy

    with ExitStack() as ctx:
        keep = ctx.enter_context(tc.tile_pool(name="keep", bufs=1))
        work = ctx.enter_context(tc.tile_pool(name="work", bufs=2))
        pools = {tag: ctx.enter_context(tc.psum_pool(name="ps_" + tag, bufs=2)) for tag in ("h", "d", "tr", "mx")}
        ctx.enter_context(tc.manual_schedule())

        gain_row = keep.tile([P, D], BF16, name="gain_row")
        nc.vector.memset(gain_row[:], 0.0)
        ones = keep.tile([P, P], BF16, name="ones")
        nc.gpsimd.memset(ones[:], 1.0)
        position = keep.tile([P, J], F32, name="position")
        nc.gpsimd.iota(position[:], [[1, J]], base=0, channel_multiplier=J, allow_small_or_imprecise_dtypes=True)
        ident_b = keep.tile([P, P], BF16, name="ident_b")
        make_identity(nc, ident_b[:])
        ident_f = keep.tile([P, P], F32, name="ident_f")
        make_identity(nc, ident_f[:])

        g_t, u_t, g2_t, x_t, w_t = {}, {}, {}, {}, {}

        def load_unit(unit, parts):
            s, b = UNITS[unit]
            g_t[unit] = work.tile([P, J, D], BF16, tag="g", name="g", bufs=2)
            u_t[unit] = work.tile([P, J, D], F32, tag="u", name="u", bufs=3)
            width = J // parts
            for part in range(parts):
                js = slice(part * width, (part + 1) * width)
                for tile, source in ((g_t[unit], grads[s]), (u_t[unit], saved[s])):
                    nc.sync.dma_start(out=tile[:, js, :], in_=source[b].rearrange("(p j) w -> p j w", j=J)[:, js, :])

        def load_grad2(b):
            g2_t[b] = work.tile([P, J, D], BF16, tag="g2", name="g2", bufs=2)
            nc.sync.dma_start(out=g2_t[b][:], in_=grad_2[b].rearrange("(p j) w -> p j w", j=J))

        def load_x(b):
            x_t[b] = work.tile([P, J, C], BF16, tag="xw", name="x_in", bufs=4)
            nc.sync.dma_start(out=x_t[b][:], in_=x[b].rearrange("(p j) c -> p j c", j=J))

        def load_w(s):
            w_t[s] = work.tile([P, J, C], BF16, tag="xw", name="w_in", bufs=4)
            nc.sync.dma_start(out=w_t[s][:], in_=W_qkv[s * D : (s + 1) * D, :].rearrange("(p j) c -> p j c", j=J))

        nc.sync.dma_start(out=gain_row[0:1, :], in_=sqk.rearrange("(o n) -> o n", o=1))
        load_unit(0, 2)
        load_grad2(0)
        load_unit(1, 1)
        load_x(1)
        load_w(K)
        load_unit(2, 1)
        load_w(V)
        load_w(Q)
        load_grad2(1)
        load_unit(3, 1)
        load_x(0)

        diag = keep.tile([P, 4, P], BF16, name="diag")
        gain_ps = pools["h"].tile([P, D], F32, tag="h", name="gain_ps")
        nc.tensor.matmul(gain_ps[:], lhsT=ones[:], rhs=gain_row[:], start=True, stop=True)

        def make_diag():
            nc.vector.tensor_tensor(
                out=diag[:],
                in0=ident_b[:].unsqueeze(1).to_broadcast([P, 4, P]),
                in1=gain_ps[:].rearrange("p (f n) -> p f n", f=4),
                op=ALU.mult,
            )

        fine_coarse = keep.tile([P, 2, 16], F32, name="fine_coarse")
        for row, first in enumerate((1.0 / (2.0 * math.pi), 1.0)):
            nc.vector.tensor_scalar(out=fine_coarse[:, row, 0:1], in0=position[:, 0:1], scalar1=0.0, scalar2=first, op0=ALU.mult, op1=ALU.add)
        for k in range(4):
            n = 1 << k
            for row, stride in enumerate((1.0, 16.0)):
                nc.vector.tensor_scalar_mul(fine_coarse[:, row, n : 2 * n], fine_coarse[:, row, 0:n], ROPE_BASE ** (-stride * n / H))
        freq = keep.tile([P, H], F32, name="freq")
        nc.vector.tensor_tensor(
            out=freq[:].rearrange("p (a c) -> p a c", a=16),
            in0=fine_coarse[:, 1, :].unsqueeze(2).to_broadcast([P, 16, 16]),
            in1=fine_coarse[:, 0, :].unsqueeze(1).to_broadcast([P, 16, 16]),
            op=ALU.mult,
        )
        turns = work.tile([P, J, H], F32, tag="A", name="turns")
        whole = work.tile([P, J, H], I32, tag="B", name="whole")
        rest = work.tile([P, J, H], F32, tag="A", name="rest")
        rest_abs = work.tile([P, J, H], F32, tag="B", name="rest_abs")
        halves = [slice(0, 2), slice(2, 4)]
        for j in range(J):
            nc.vector.tensor_scalar_mul(turns[:, j, :], freq[:], position[:, j : j + 1])
        for js in halves:
            nc.vector.tensor_copy(out=whole[:, js, :], in_=turns[:, js, :])

        def take_rest(half):
            js = halves[half]
            nc.vector.tensor_tensor(out=rest[:, js, :], in0=turns[:, js, :], in1=whole[:, js, :], op=ALU.subtract)

        def take_abs(half):
            js = halves[half]
            nc.vector.scalar_tensor_tensor(out=rest_abs[:, js, :], in0=rest[:, js, :], scalar=-1.0, in1=rest[:, js, :], op0=ALU.mult, op1=ALU.max)

        take_rest(0)
        make_diag()
        take_abs(0)
        take_rest(1)
        sin_t = keep.tile([P, J, H], F32, name="sin_t")
        cos_t = keep.tile([P, J, H], F32, name="cos_t")
        warm = keep.tile([P, 1], F32, name="warm")
        nc.scalar.activation(out=warm[:], in_=position[:, 0:1], func=ACT.Sin, scale=0.0)

        def tables(half):
            js = halves[half]
            nc.scalar.activation(out=cos_t[:, js, :], in_=rest_abs[:, js, :], func=ACT.Sin, scale=-2.0 * math.pi, bias=math.pi / 2.0)
            nc.scalar.activation(out=sin_t[:, js, :], in_=rest[:, js, :], func=ACT.Sin, scale=2.0 * math.pi)

        def mx_operand(name, width):
            codes = keep.tile([P, width], U32, name=name + "_c", align_bytes=64)
            scales = keep.tile([P, width], U8, name=name + "_s", align_bytes=64)
            return codes, scales

        x_q = [mx_operand("x%d" % b, C) for b in range(B)]
        w_q = [mx_operand("w%d" % s, C) for s in range(3)]
        tok_q = [[mx_operand("t%d%d" % (s, b), D) for b in range(B)] for s in range(3)]
        fea_q = [[mx_operand("f%d%d" % (s, b), D) for b in range(B)] for s in range(3)]

        def quantize(operand, lo, width, values, fmt):
            nc.vector.quantize_mx(out=operand[0][:, lo : lo + width].bitcast(fmt), scales=operand[1][:, lo : lo + width], in_=values)

        def interleave(copy, out, in_):
            copy(out=out.rearrange("p (c i t) -> p c t i", i=4, t=J), in_=in_.rearrange("p t (c i) -> p c t i", i=4))

        staged = {}

        def slots_of(piece):
            kind, index, half = piece
            cols = slice(half * D, (half + 1) * D)
            if kind == "x":
                return x_t[index][:, :, cols]
            if kind == "w":
                return w_t[index][:, :, cols]
            return g2_t[index][:] if kind == "v" else z_t[index][:]

        def scalar_copy(piece):
            staged[piece] = work.tile([P, J * D], BF16, tag="stage", name="stage", bufs=4, align_bytes=64)
            interleave(by_scalar, staged[piece][:], slots_of(piece))

        def quantize_piece(piece):
            kind, index, half = piece
            values = staged[piece][:]
            if kind == "x":
                quantize(x_q[index], half * D, D, values, E4M3)
            elif kind == "w":
                quantize(w_q[index], half * D, D, values, E4M3)
            else:
                s, b = (V, index) if kind == "v" else UNITS[index]
                quantize(tok_q[s][b], 0, D, values, E5M2)

        gpsimd_todo = list(GPSIMD_COPIES)
        gpsimd_done = []

        def window():
            if gpsimd_done:
                quantize_piece(gpsimd_done.pop())
            if gpsimd_todo:
                piece = gpsimd_todo.pop(0)
                staged[piece] = work.tile([P, J * D], BF16, tag="gs", name="gs", bufs=1, align_bytes=64)
                nc.gpsimd.tensor_scalar(
                    out=staged[piece][:].rearrange("p (c t) -> p c t", t=J),
                    in0=slots_of(piece).rearrange("p t c -> p c t"),
                    scalar1=1.0, scalar2=0.0, op0=ALU.mult, op1=ALU.add,
                )
                gpsimd_done.append(piece)

        z_t, g_tr, g_sb, h_t, ss, rr, rt, dots, alphas, d_rows, a_t, b_t = {}, {}, {}, {}, {}, {}, {}, {}, {}, {}, {}, {}

        def slot(i, jj):
            return 2 * (i % 2) + jj

        def grad_transpose(i, parts=1):
            g_tr[i] = []
            for part in range(parts):
                tr = pools["tr"].tile([P, 2 // parts, 4, P], BF16, tag="tr", name="gtr")
                for jj in range(2 // parts):
                    for f in range(4):
                        block = g_t[i // 2][:, slot(i, 2 * part // parts + jj), f * P : (f + 1) * P]
                        nc.tensor.transpose(tr[:, jj, f, :], block, ident_b[:])
                g_tr[i].append(tr)

        def grad_copy(i, copy):
            g_sb[i] = work.tile([P, 2, 4, P], BF16, tag="gT", name="gT", bufs=2)
            n = 2 // len(g_tr[i])
            for part, tr in enumerate(g_tr[i]):
                copy(out=g_sb[i][:, part * n : (part + 1) * n, :, :], in_=tr[:])

        def gain_matmuls(i, jj, out, stop):
            for f in range(4):
                nc.tensor.matmul(
                    out[:, f * P : (f + 1) * P], lhsT=g_sb[i][:, jj, f, :], rhs=diag[:, f, :], start=(f == 0), stop=(stop and f == 3)
                )

        def apply_gain(i):
            for jj in range(2):
                h_t[i, jj] = pools["h"].tile([P, D], F32, tag="h", name="h")
                gain_matmuls(i, jj, h_t[i, jj], True)

        def squares(i):
            ss[i] = work.tile([P, 2], F32, tag="ss", name="ss", bufs=3)
            for jj in range(2):
                unread = work.tile([P, D], BF16, tag="sq", name="sq")
                nc.scalar.activation(out=unread[:], in_=u_t[i // 2][:, slot(i, jj), :], func=ACT.Square, accum_out=ss[i][:, jj : jj + 1])

        def norm_square_reciprocal(i):
            rr[i] = work.tile([P, 2], F32, tag="rr", name="rr", bufs=3)
            nc.vector.reciprocal(rr[i][:], ss[i][:])

        def norm_reciprocal(i):
            rt[i] = work.tile([P, 2], F32, tag="rt", name="rt", bufs=3)
            nc.scalar.activation(out=rt[i][:], in_=rr[i][:], func=ACT.Sqrt)

        def dot(i, jj):
            if jj == 0:
                dots[i] = work.tile([P, 2], F32, tag="dots", name="dots", bufs=3)
            unread = work.tile([P, D], F32, tag="prod", name="prod")
            nc.vector.scalar_tensor_tensor(
                out=unread[:], in0=h_t[i, jj][:], scalar=1.0, in1=u_t[i // 2][:, slot(i, jj), :],
                op0=ALU.mult, op1=ALU.mult, accum_out=dots[i][:, jj : jj + 1],
            )

        def alpha(i):
            alphas[i] = work.tile([P, 2], F32, tag="nal", name="nal", bufs=3)
            for jj in range(2):
                col = slice(jj, jj + 1)
                nc.vector.tensor_scalar(out=alphas[i][:, col], in0=dots[i][:, col], scalar1=rr[i][:, col], scalar2=-1.0, op0=ALU.mult, op1=ALU.mult)

        def project(i, jj):
            u_rows, col = u_t[i // 2][:, slot(i, jj), :], slice(jj, jj + 1)
            if i in TENSOR_STEPS:
                alpha_diag = work.tile([P, P], F32, tag="alpha_diag", name="alpha_diag")
                nc.scalar.activation(out=alpha_diag[:], in_=ident_f[:], func=ACT.Copy, scale=alphas[i][:, col])
                d_ps = pools["d"].tile([P, D], F32, tag="d", name="d_ps")
                gain_matmuls(i, jj, d_ps, False)
                nc.tensor.matmul(d_ps[:], lhsT=alpha_diag[:], rhs=u_rows, start=False, stop=True)
                d_rows[i, jj] = d_ps[:]
            else:
                d_sb = work.tile([P, D], F32, tag="d", name="d_sb", bufs=4)
                nc.vector.scalar_tensor_tensor(out=d_sb[:], in0=u_rows, scalar=alphas[i][:, col], in1=h_t[i, jj][:], op0=ALU.mult, op1=ALU.add)
                d_rows[i, jj] = d_sb[:]

        def times(i, table, store, tag, lo=0, hi=H):
            if lo == 0:
                store[i] = work.tile([P, 2, D], F32, tag=tag, name=tag)
            for jj in range(2):
                nc.vector.scalar_tensor_tensor(
                    out=store[i][:, jj, :].rearrange("p (h w) -> p h w", h=2)[:, :, lo:hi],
                    in0=d_rows[i, jj].rearrange("p (h w) -> p h w", h=2)[:, :, lo:hi],
                    scalar=rt[i][:, jj : jj + 1],
                    in1=table[:, jj, lo:hi].unsqueeze(1).to_broadcast([P, 2, hi - lo]),
                    op0=ALU.mult, op1=ALU.mult,
                )

        def times_cos(i, lo=0, hi=H):
            times(i, cos_t[:, halves[i % 2], :], a_t, "A", lo, hi)

        def times_sin(i, lo=0, hi=H):
            times(i, sin_t[:, halves[i % 2], :], b_t, "B", lo, hi)

        def rotate(i, lo=0, hi=H):
            if i % 2 == 0:
                z_t[i // 2] = work.tile([P, J, D], BF16, tag="z", name="z", align_bytes=64)
            js = halves[i % 2]
            z, a, b = z_t[i // 2], a_t[i], b_t[i]
            one, two = slice(lo, hi), slice(H + lo, H + hi)
            nc.vector.tensor_tensor(out=z[:, js, one], in0=a[:, :, one], in1=b[:, :, two], op=ALU.add)
            nc.vector.tensor_tensor(out=z[:, js, two], in0=a[:, :, two], in1=b[:, :, one], op=ALU.subtract)

        z_tr, z_fea = {}, {}

        def step_key(i):
            return UNITS[i // 2] + (i % 2,)

        def fea_transpose(key):
            s, b, half = key
            rows = g2_t[b] if s == V else z_t[UNITS.index((s, b))]
            words = rows[:].rearrange("p j w -> p (j w)").bitcast(F32)
            tr = pools["tr"].tile([P, 2, 2, P], F32, tag="tr", name="ztr")
            for jj in range(2):
                lo = (2 * half + jj) * H
                for e in range(2):
                    nc.tensor.transpose(tr[:, jj, e, :], words[:, lo + e : lo + H : 2], ident_f[:])
            z_tr[key] = tr

        def fea_copy(key, copy):
            z_fea[key] = work.tile([P, J * H], BF16, tag="fst", name="fst", bufs=3, align_bytes=64)
            copy(
                out=z_fea[key][:].bitcast(F32).rearrange("p (j t e) -> p j t e", j=2, e=2),
                in_=z_tr[key][:].rearrange("p j e t -> p j t e"),
            )

        def fea_quantize(key):
            s, b, half = key
            quantize(fea_q[s][b], half * H, H, z_fea[key][:], E5M2)

        def operands(item):
            kind, index, n = item
            if kind == "dw":
                row = index * D + n * P
                return tok_q[index], x_q, n * P, out_1[row : row + P, :]
            order = (V, Q, K)
            rows = out_0[index].rearrange("(p j) c -> p j c", j=J)[:, n, :]
            return [fea_q[s][index] for s in order], [w_q[s] for s in order], n * P, rows

        def passes(item, accs):
            lhs, rhs, lo, rows = operands(item)
            for n in range(2):
                cols = slice(n * D, (n + 1) * D)
                for k in range(len(lhs)):
                    nc.tensor.matmul_mx(
                        out=accs[n][:],
                        lhsT=lhs[k][0][:, lo : lo + P].bitcast(E5M2),
                        lhsT_scale=lhs[k][1][:, lo : lo + P],
                        rhs=rhs[k][0][:, cols].bitcast(E4M3),
                        rhs_scale=rhs[k][1][:, cols],
                        start=(k == 0),
                        stop=(k == len(lhs) - 1),
                    )

        def output_tile(item, tag, stores=1):
            accs = [pools[tag].tile([P, D], F32, tag=tag, name="acc") for n in range(2)]
            passes(item, accs)
            rows = operands(item)[3]
            o = work.tile([P, C], F32, tag="o", name="o", bufs=5)
            for n in range(2):
                cols = slice(n * D, (n + 1) * D)
                copy = by_vector if n in VECTOR_BANKS.get(item, ()) else by_scalar
                copy(out=o[:, cols], in_=accs[n][:])
                if stores == 2:
                    nc.sync.dma_start(out=rows[:, cols], in_=o[:, cols])
            if stores == 1:
                nc.sync.dma_start(out=rows, in_=o[:])

        grad_transpose(0, 2)
        grad_copy(0, by_scalar)
        apply_gain(0)
        grad_transpose(1)
        squares(0)
        tables(0)
        dot(0, 0)
        dot(0, 1)
        norm_square_reciprocal(0)
        take_abs(1)
        alpha(0)
        grad_copy(1, by_vector)
        project(0, 0)
        project(0, 1)
        apply_gain(1)
        squares(1)
        tables(1)
        norm_reciprocal(0)
        norm_square_reciprocal(1)
        norm_reciprocal(1)

        window()
        to_quantize = []
        for i in range(LAST):
            nxt, pre = i + 1, i + 2
            grad2_keys = [(V, b, half) for b, half in GRAD2_HALVES.get(i, [])]
            if pre < STEPS:
                grad_transpose(pre)
            dot(nxt, 0)
            dot(nxt, 1)
            if pre < STEPS:
                grad_copy(pre, by_vector if pre == VECTOR_COPY_STEP else by_scalar)
            for item, tag in EARLY_TILES.get(i, []):
                output_tile(item, tag)
            if i > 0:
                norm_reciprocal(nxt)
            for key in grad2_keys:
                fea_transpose(key)
                fea_copy(key, by_scalar)
            alpha(nxt)
            if i > 0:
                fea_transpose(step_key(i - 1))
            if pre < STEPS:
                apply_gain(pre)
            project(nxt, 0)
            project(nxt, 1)
            if pre < STEPS:
                squares(pre)
            times_cos(i)
            times_sin(i)
            for piece in to_quantize:
                quantize_piece(piece)
            for key in grad2_keys:
                fea_quantize(key)
            rotate(i)
            if i > 0:
                fea_copy(step_key(i - 1), by_vector if i - 1 == VECTOR_COPY_STEP else by_scalar)
                fea_quantize(step_key(i - 1))
            window()
            for item, tag in LATE_TILES.get(i, []):
                output_tile(item, tag)
            to_quantize = SCALAR_COPIES.get(i, [])
            for piece in to_quantize:
                scalar_copy(piece)
            if pre < STEPS:
                norm_square_reciprocal(pre)

        stage = work.tile([P, J * D], BF16, tag="stage", name="stage", bufs=4, align_bytes=64)

        def block_copy(m):
            interleave(by_vector, stage[:, m * D : (m + 1) * D], z_t[3][:, :, m * P : (m + 1) * P])

        def block_quantize(m):
            quantize(tok_q[K][1], m * P, P, stage[:, m * D : (m + 1) * D], E5M2)

        fea_transpose(step_key(LAST - 1))
        fea_copy(step_key(LAST - 1), by_scalar)
        times_cos(LAST, 0, P)
        times_sin(LAST, 0, P)
        times_sin(LAST, P, H)
        rotate(LAST, 0, P)
        fea_quantize(step_key(LAST - 1))
        block_copy(0)
        block_copy(2)
        times_cos(LAST, P, H)
        block_quantize(0)
        rotate(LAST, P, H)
        output_tile(("dw", Q, 0), "d")
        output_tile(("dx", 1, 1), "h")
        output_tile(("dx", 1, 0), "d")
        block_quantize(2)
        output_tile(("dw", K, 0), "mx")
        block_copy(3)
        block_quantize(3)
        fea_transpose(step_key(LAST))
        block_copy(1)
        fea_copy(step_key(LAST), by_scalar)
        output_tile(("dw", K, 2), "h")
        output_tile(("dw", K, 3), "d")
        fea_quantize(step_key(LAST))
        block_quantize(1)
        output_tile(("dw", K, 1), "tr")
        output_tile(("dx", 1, 3), "d")
        output_tile(("dx", 1, 2), "d", stores=2)
